import numpy as np
import ml_dtypes


def mxq(x, axis, fmt="e4m3"):
    dtype, down = {"e4m3": (ml_dtypes.float8_e4m3fn, 7), "e5m2": (ml_dtypes.float8_e5m2, 14)}[fmt]
    v = np.moveaxis(np.asarray(x, np.float32).astype(ml_dtypes.bfloat16).astype(np.float64), axis, -1)
    blocks = v.reshape(v.shape[:-1] + (-1, 32))
    amax = np.abs(blocks).max(-1, keepdims=True)
    byte = np.maximum(np.where(amax > 0, np.frexp(amax)[1] - 1 + 127, 0) - down, 1)
    scale = np.exp2(byte - 127.0)
    codes = (blocks / scale).astype(np.float32).astype(dtype).astype(np.float64)
    return np.moveaxis((codes * scale).reshape(v.shape), -1, axis)


WIDE = False


def mx_kscale(k):
    if not WIDE:
        return np.ones(k)
    levels = np.array([10, -10, 5, -5, 0])
    a = np.random.permutation(np.resize(levels, k // 512 * 4)).reshape(k // 512, 4)
    idx = np.arange(k)
    return np.exp2(a[idx // 512, idx % 128 // 32])


BF16 = ml_dtypes.bfloat16


def bf(x):
    return np.asarray(x, np.float32).astype(BF16)


def f64(x):
    return np.asarray(x).astype(np.float64)


B, IN, H, G, GA, GB = 4096, 1024, 512, 6, 4, 2
EPS = 1e-5


def layer_norm(v, g, b):
    mu = v.mean(-1, keepdims=True)
    var = np.square(v - mu).mean(-1, keepdims=True)
    return (v - mu) / np.sqrt(var + EPS) * g + b


def sigmoid(v):
    return 1.0 / (1.0 + np.exp(-v))


def setup_inputs():
    s = mx_kscale(IN)
    return {"x": bf(np.random.standard_normal((B, IN)) * s),
            "h": bf(np.random.standard_normal((B, H))),
            "c": bf(np.tanh(1.4 * np.random.standard_normal((B, H)))),
            "W_u": bf(np.random.standard_normal((H, H)) / np.sqrt(H)),
            "U_u": bf(np.random.standard_normal((H, IN)) / np.sqrt(IN) / s),
            "ln_gamma": bf(1.0 + 0.1 * np.random.standard_normal((GB, H))),
            "ln_beta": bf(0.2 * np.random.standard_normal((GB, H)))}


def reference(x, h, c, W_u, U_u, ln_gamma, ln_beta):
    g_uh, g_ux = f64(ln_gamma)
    b_uh, b_ux = f64(ln_beta)
    hf = f64(h)
    u = sigmoid(layer_norm(mxq(hf, 1, "e4m3") @ mxq(f64(W_u), 1, "e4m3").T, g_uh, b_uh)
                + layer_norm(mxq(f64(x), 1, "e4m3") @ mxq(f64(U_u), 1, "e4m3").T, g_ux, b_ux))
    return (1.0 - u) * hf + u * f64(c)

@@ -1,0 +1,266 @@
+from contextlib import ExitStack
+
+import concourse.mybir as mybir
+from concourse.masks import make_identity
+
+F32 = mybir.dt.float32
+BF16 = mybir.dt.bfloat16
+U32 = mybir.dt.uint32
+U8 = mybir.dt.uint8
+FP8X4 = mybir.dt.float8_e4m3fn_x4
+ALU = mybir.AluOpType
+ACT = mybir.ActivationFunctionType
+
+P = 128
+B, IN, H = 4096, 1024, 512
+NT = B // P
+CH = 4
+NCH = NT // CH
+EPS = 1e-5
+FLOPS = 2 * B * H * (H + IN)
+MANUAL = False
+
+
+def tile_layernormgrucell_pb_t_kernel(tc, x, h, c, W_u, U_u, ln_gamma, ln_beta, out):
+    nc = tc.nc
+    with ExitStack() as ctx:
+        const = ctx.enter_context(tc.tile_pool(name="const", bufs=1))
+        xin = ctx.enter_context(tc.tile_pool(name="xin", bufs=4))
+        hin = ctx.enter_context(tc.tile_pool(name="hin", bufs=NCH))
+        cin = ctx.enter_context(tc.tile_pool(name="cin", bufs=4))
+        grp = ctx.enter_context(tc.tile_pool(name="grp", bufs=2))
+        cod = ctx.enter_context(tc.tile_pool(name="cod", bufs=3))
+        wrk = ctx.enter_context(tc.tile_pool(name="wrk", bufs=3))
+        dpl = ctx.enter_context(tc.tile_pool(name="dpl", bufs=6))
+        sml = ctx.enter_context(tc.tile_pool(name="sml", bufs=4))
+        opl = ctx.enter_context(tc.tile_pool(name="opl", bufs=3))
+        ps_t = ctx.enter_context(tc.psum_pool(name="ps_t", bufs=1))
+        ps_p = ctx.enter_context(tc.psum_pool(name="ps_p", bufs=2))
+
+        xv = x.rearrange("(p t) k -> p t k", t=NT)
+        hv = h.rearrange("(p t) k -> p t k", t=NT)
+        cv = c.rearrange("(p t) k -> p t k", t=NT)
+        ov = out.rearrange("(p t) f -> p t f", t=NT)
+
+        x_ch, h_ch, c_ch = {}, {}, {}
+
+        def load_h(ci):
+            t = hin.tile([P, CH, H], BF16, name="h_ch", tag="h_ch")
+            nc.sync.dma_start(out=t[:], in_=hv[:, ci * CH:(ci + 1) * CH, :])
+            h_ch[ci] = t
+
+        def load_x(ci):
+            t = xin.tile([P, CH, IN], BF16, name="x_ch", tag="x_ch")
+            nc.sync.dma_start(out=t[:], in_=xv[:, ci * CH:(ci + 1) * CH, :])
+            x_ch[ci] = t
+
+        def load_c(ci):
+            t = cin.tile([P, CH, H], BF16, name="c_ch", tag="c_ch")
+            nc.sync.dma_start(out=t[:], in_=cv[:, ci * CH:(ci + 1) * CH, :])
+            c_ch[ci] = t
+
+        w_raw = const.tile([P, 4, H], BF16, name="w_raw")
+        nc.sync.dma_start(out=w_raw[:], in_=W_u.rearrange("(b p) k -> p b k", p=P))
+        load_h(0)
+        u_raw = const.tile([P, 4, IN], BF16, name="u_raw")
+        nc.sync.dma_start(out=u_raw[:], in_=U_u.rearrange("(b p) k -> p b k", p=P))
+        load_x(0)
+        gam = const.tile([P, 2 * H], BF16, name="gam")
+        nc.sync.dma_start(out=gam[:], in_=ln_gamma.rearrange("g f -> (g f)").partition_broadcast(P))
+        bet = const.tile([P, 2 * H], BF16, name="bet")
+        nc.sync.dma_start(out=bet[:], in_=ln_beta.rearrange("g f -> (g f)").partition_broadcast(P))
+        load_c(0)
+        for ci in (1, 2):
+            load_h(ci)
+            load_x(ci)
+            load_c(ci)
+
+        ident = const.tile([P, P], F32, name="ident")
+        make_identity(nc, ident[:])
+        mhalf = const.tile([P, 2], F32, name="mhalf")
+        nc.gpsimd.memset(mhalf[:], -0.5)
+
+        gw = const.tile([P, 3, 4 * H], BF16, name="gw", align_bytes=64)
+        wc = const.tile([P, 3, H], U32, name="wc", align_bytes=64)
+        ws = const.tile([P, 3, H], U8, name="ws", align_bytes=64)
+        gw_w = gw[:].bitcast(F32)
+        n_bank = 0
+        for s in range(3):
+            raw_w = (w_raw if s == 0 else u_raw)[:].bitcast(F32)
+            g = max(s - 1, 0)
+            for j in range(2):
+                bank = ps_t.tile([P, 512], F32, name="xt", tag="xt%d" % (n_bank % 2))
+                for u in range(2):
+                    for fl in range(2):
+                        nc.tensor.transpose(
+                            bank[:, u * 256 + fl * P:u * 256 + (fl + 1) * P],
+                            raw_w[:, 2 * j + fl, (2 * g + u) * P:(2 * g + u + 1) * P],
+                            ident[:],
+                        )
+                dst = gw_w[:, s, j * 512:(j + 1) * 512].rearrange("p (f u) -> p f u", u=2)
+                src = bank[:].rearrange("p (u f) -> p f u", u=2)
+                if n_bank % 2 == 0:
+                    nc.scalar.copy(out=dst, in_=src)
+                else:
+                    nc.vector.tensor_copy(out=dst, in_=src)
+                n_bank += 1
+        bs = const.tile([P, H], F32, name="bs")
+        nc.vector.tensor_tensor(out=bs[:], in0=bet[:, 0:H], in1=bet[:, H:2 * H], op=ALU.add)
+        for s in range(3):
+            nc.vector.quantize_mx(out=wc[:, s, :].bitcast(FP8X4), scales=ws[:, s, :], in_=gw[:, s, :])
+
+        banks, gx_t, gh_t, cx_t, sx_t, chh_t, shh_t = {}, {}, {}, {}, {}, {}, {}
+        p0_t, p1_t, q_t, nm_t, ss_t, r_t, a_t, b_t, d_t, o_t = {}, {}, {}, {}, {}, {}, {}, {}, {}, {}
+
+        def tr(J):
+            if not 0 <= J < NT // 2:
+                return
+            ht = ps_t.tile([P, 512], F32, name="ht", tag="ht")
+            xts = []
+            for tau in range(2):
+                i = 2 * J + tau
+                xw = x_ch[i // CH][:].bitcast(F32)
+                hw = h_ch[i // CH][:].bitcast(F32)
+                xt = ps_t.tile([P, 512], F32, name="xt", tag="xt%d" % tau)
+                for wb in range(4):
+                    nc.tensor.transpose(xt[:, wb * P:(wb + 1) * P], xw[:, i % CH, wb * P:(wb + 1) * P], ident[:])
+                for u in range(2):
+                    nc.tensor.transpose(ht[:, (2 * tau + u) * P:(2 * tau + u + 1) * P], hw[:, i % CH, u * P:(u + 1) * P], ident[:])
+                xts.append(xt)
+            banks[J] = (xts[0], xts[1], ht)
+            gx_t[J] = grp.tile([P, 2, IN], BF16, name="gx", tag="gx", align_bytes=64)
+            gh_t[J] = grp.tile([P, 2, H], BF16, name="gh", tag="gh", align_bytes=64)
+
+        def ev(J, part):
+            if not 0 <= J < NT // 2:
+                return
+            gxw = gx_t[J][:].bitcast(F32)
+            src = banks[J][part][:].rearrange("p (g u r) -> p g r u", g=2, u=2)
+            nc.scalar.copy(out=gxw[:, part, :].rearrange("p (g r u) -> p g r u", g=2, u=2), in_=src)
+            if part == 0:
+                ghw = gh_t[J][:].bitcast(F32)
+                srch = banks[J][2][:].rearrange("p (t u r) -> p t r u", t=2, u=2)
+                nc.scalar.copy(out=ghw.rearrange("p t (r u) -> p t r u", u=2), in_=srch)
+
+        def qz(J):
+            if not 0 <= J < NT // 2:
+                return
+            cx = cod.tile([P, 512], U32, name="cx", tag="cx", align_bytes=64)
+            sx = cod.tile([P, 512], U8, name="sx", tag="sx", align_bytes=64)
+            chh = cod.tile([P, 256], U32, name="chh", tag="chh", align_bytes=64)
+            shh = cod.tile([P, 256], U8, name="shh", tag="shh", align_bytes=64)
+            nc.vector.quantize_mx(out=chh[:].bitcast(FP8X4), scales=shh[:], in_=gh_t[J][:].rearrange("p t k -> p (t k)"))
+            nc.vector.quantize_mx(out=cx[:].bitcast(FP8X4), scales=sx[:], in_=gx_t[J][:].rearrange("p t k -> p (t k)"))
+            cx_t[J], sx_t[J], chh_t[J], shh_t[J] = cx, sx, chh, shh
+
+        def mm(i):
+            if not 0 <= i < NT:
+                return
+            J, tau = i // 2, i % 2
+            p0 = ps_p.tile([P, H], F32, name="p0", tag="p0")
+            p1 = ps_p.tile([P, H], F32, name="p1", tag="p1")
+            hs = slice(tau * P, (tau + 1) * P)
+            nc.tensor.matmul_mx(out=p0[:], lhsT=chh_t[J][:, hs].bitcast(FP8X4), lhsT_scale=shh_t[J][:, hs],
+                                rhs=wc[:, 0, :].bitcast(FP8X4), rhs_scale=ws[:, 0, :], start=True, stop=True)
+            for g in range(2):
+                xs = slice(tau * 256 + g * P, tau * 256 + (g + 1) * P)
+                nc.tensor.matmul_mx(out=p1[:], lhsT=cx_t[J][:, xs].bitcast(FP8X4), lhsT_scale=sx_t[J][:, xs],
+                                    rhs=wc[:, 1 + g, :].bitcast(FP8X4), rhs_scale=ws[:, 1 + g, :],
+                                    start=(g == 0), stop=(g == 1))
+            p0_t[i], p1_t[i] = p0, p1
+
+        def st(i):
+            if not 0 <= i < NT:
+                return
+            nm = sml.tile([P, 2], F32, name="nm", tag="nm")
+            ss = sml.tile([P, 2], F32, name="ss", tag="ss")
+            q0 = wrk.tile([P, H], F32, name="q0", tag="q0")
+            q1 = wrk.tile([P, H], F32, name="q1", tag="q1")
+            nc.scalar.activation(out=q0[:], in_=p0_t[i][:], func=ACT.Identity, scale=-1.0 / H, accum_out=nm[:, 0:1])
+            nc.scalar.activation(out=q1[:], in_=p1_t[i][:], func=ACT.Identity, scale=-1.0 / H, accum_out=nm[:, 1:2])
+            nc.scalar.activation(out=q0[:], in_=q0[:], func=ACT.Square, scale=-1.0 * H, bias=nm[:, 0:1], accum_out=ss[:, 0:1])
+            nc.scalar.activation(out=q1[:], in_=q1[:], func=ACT.Square, scale=-1.0 * H, bias=nm[:, 1:2], accum_out=ss[:, 1:2])
+            nm_t[i], ss_t[i] = nm, ss
+
+        def rs(i):
+            if not 0 <= i < NT:
+                return
+            v = sml.tile([P, 2], F32, name="v", tag="v")
+            r = sml.tile([P, 2], F32, name="r", tag="r")
+            nc.gpsimd.tensor_scalar(out=v[:], in0=ss_t[i][:], scalar1=1.0 / H, scalar2=EPS, op0=ALU.mult, op1=ALU.add)
+            nc.gpsimd.tensor_tensor(out=r[:], in0=v[:], in1=mhalf[:], op=ALU.pow)
+            r_t[i] = r
+
+        def dd(i):
+            if not 0 <= i < NT:
+                return
+            dt_ = dpl.tile([P, H], F32, name="d", tag="d")
+            nc.gpsimd.tensor_tensor(out=dt_[:], in0=c_ch[i // CH][:, i % CH, :], in1=h_ch[i // CH][:, i % CH, :], op=ALU.subtract)
+            d_t[i] = dt_
+
+        def ab(i):
+            if not 0 <= i < NT:
+                return
+            a = wrk.tile([P, H], F32, name="a", tag="a")
+            b = wrk.tile([P, H], F32, name="b", tag="b", bufs=4)
+            nc.vector.scalar_tensor_tensor(out=a[:], in0=p0_t[i][:], scalar=nm_t[i][:, 0:1], in1=gam[:, 0:H], op0=ALU.add, op1=ALU.mult)
+            nc.vector.scalar_tensor_tensor(out=b[:], in0=p1_t[i][:], scalar=nm_t[i][:, 1:2], in1=gam[:, H:2 * H], op0=ALU.add, op1=ALU.mult)
+            a_t[i], b_t[i] = a, b
+
+        def yz(i):
+            if not 0 <= i < NT:
+                return
+            a, b, r = a_t[i], b_t[i], r_t[i]
+            nc.vector.scalar_tensor_tensor(out=a[:], in0=a[:], scalar=r[:, 0:1], in1=bs[:], op0=ALU.mult, op1=ALU.add)
+            nc.vector.scalar_tensor_tensor(out=b[:], in0=b[:], scalar=r[:, 1:2], in1=a[:], op0=ALU.mult, op1=ALU.add)
+
+        def sg(i):
+            if not 0 <= i < NT:
+                return
+            nc.scalar.activation(out=b_t[i][:], in_=b_t[i][:], func=ACT.Sigmoid)
+
+        def bl(i):
+            if not 0 <= i < NT:
+                return
+            J, tau = i // 2, i % 2
+            if tau == 0:
+                o_t[J] = opl.tile([P, 2, H], F32, name="o", tag="o")
+            o = o_t[J]
+            nc.vector.tensor_tensor(out=o[:, tau, :], in0=b_t[i][:], in1=d_t[i][:], op=ALU.mult)
+            nc.vector.tensor_tensor(out=o[:, tau, :], in0=o[:, tau, :], in1=h_ch[i // CH][:, i % CH, :], op=ALU.add)
+            if tau == 1:
+                nc.sync.dma_start(out=ov[:, 2 * J:2 * J + 2, :], in_=o[:])
+
+        if MANUAL:
+            ctx.enter_context(tc.manual_schedule())
+
+        tr(0)
+        ev(0, 0)
+        ev(0, 1)
+        tr(1)
+        qz(0)
+        ev(1, 0)
+        ev(1, 1)
+        mm(0)
+        dd(0)
+        dd(1)
+
+        for i in range(NT + 2):
+            if i % CH == 0 and i // CH + 3 < NCH:
+                load_h(i // CH + 3)
+                load_x(i // CH + 3)
+                load_c(i // CH + 3)
+            yz(i - 1)
+            st(i)
+            rs(i)
+            dd(i + 2)
+            sg(i - 1)
+            bl(i - 2)
+            ab(i)
+            mm(i + 1)
+            if i % 2 == 0:
+                tr(i // 2 + 2)
+                ev(i // 2 + 2, 0)
+                qz(i // 2 + 1)
+            else:
+                ev((i - 1) // 2 + 2, 1)

@@ -7,6 +7,7 @@ F32 = mybir.dt.float32
 BF16 = mybir.dt.bfloat16
 U32 = mybir.dt.uint32
 U8 = mybir.dt.uint8
+I32 = mybir.dt.int32
 FP8X4 = mybir.dt.float8_e4m3fn_x4
 ALU = mybir.AluOpType
 ACT = mybir.ActivationFunctionType
@@ -18,7 +19,7 @@ CH = 4
 NCH = NT // CH
 EPS = 1e-5
 FLOPS = 2 * B * H * (H + IN)
-MANUAL = False
+MANUAL = True
 
 
 def tile_layernormgrucell_pb_t_kernel(tc, x, h, c, W_u, U_u, ln_gamma, ln_beta, out):
@@ -30,12 +31,13 @@ def tile_layernormgrucell_pb_t_kernel(tc, x, h, c, W_u, U_u, ln_gamma, ln_beta, 
         cin = ctx.enter_context(tc.tile_pool(name="cin", bufs=4))
         grp = ctx.enter_context(tc.tile_pool(name="grp", bufs=2))
         cod = ctx.enter_context(tc.tile_pool(name="cod", bufs=3))
-        wrk = ctx.enter_context(tc.tile_pool(name="wrk", bufs=3))
-        dpl = ctx.enter_context(tc.tile_pool(name="dpl", bufs=6))
-        sml = ctx.enter_context(tc.tile_pool(name="sml", bufs=4))
+        wrk = ctx.enter_context(tc.tile_pool(name="wrk", bufs=4))
+        dpl = ctx.enter_context(tc.tile_pool(name="dpl", bufs=7))
+        sml = ctx.enter_context(tc.tile_pool(name="sml", bufs=5))
         opl = ctx.enter_context(tc.tile_pool(name="opl", bufs=3))
         ps_t = ctx.enter_context(tc.psum_pool(name="ps_t", bufs=1))
         ps_p = ctx.enter_context(tc.psum_pool(name="ps_p", bufs=2))
+        ps_c = ctx.enter_context(tc.psum_pool(name="ps_c", bufs=1))
 
         xv = x.rearrange("(p t) k -> p t k", t=NT)
         hv = h.rearrange("(p t) k -> p t k", t=NT)
@@ -65,10 +67,10 @@ def tile_layernormgrucell_pb_t_kernel(tc, x, h, c, W_u, U_u, ln_gamma, ln_beta, 
         u_raw = const.tile([P, 4, IN], BF16, name="u_raw")
         nc.sync.dma_start(out=u_raw[:], in_=U_u.rearrange("(b p) k -> p b k", p=P))
         load_x(0)
-        gam = const.tile([P, 2 * H], BF16, name="gam")
-        nc.sync.dma_start(out=gam[:], in_=ln_gamma.rearrange("g f -> (g f)").partition_broadcast(P))
-        bet = const.tile([P, 2 * H], BF16, name="bet")
-        nc.sync.dma_start(out=bet[:], in_=ln_beta.rearrange("g f -> (g f)").partition_broadcast(P))
+        zt = const.tile([P, 3, H], BF16, name="zt")
+        nc.vector.memset(zt[:].bitcast(I32), 0)
+        nc.sync.dma_start(out=zt[0:1, 0:2, :], in_=ln_gamma.rearrange("(o g) f -> o g f", o=1))
+        nc.sync.dma_start(out=zt[0:2, 2, :], in_=ln_beta)
         load_c(0)
         for ci in (1, 2):
             load_h(ci)
@@ -77,6 +79,8 @@ def tile_layernormgrucell_pb_t_kernel(tc, x, h, c, W_u, U_u, ln_gamma, ln_beta, 
 
         ident = const.tile([P, P], F32, name="ident")
         make_identity(nc, ident[:])
+        ones = const.tile([P, P], BF16, name="ones")
+        nc.vector.memset(ones[:], 1.0)
         mhalf = const.tile([P, 2], F32, name="mhalf")
         nc.gpsimd.memset(mhalf[:], -0.5)
 
@@ -104,8 +108,13 @@ def tile_layernormgrucell_pb_t_kernel(tc, x, h, c, W_u, U_u, ln_gamma, ln_beta, 
                 else:
                     nc.vector.tensor_copy(out=dst, in_=src)
                 n_bank += 1
-        bs = const.tile([P, H], F32, name="bs")
-        nc.vector.tensor_tensor(out=bs[:], in0=bet[:, 0:H], in1=bet[:, H:2 * H], op=ALU.add)
+        gam = const.tile([P, 2 * H], F32, name="gam")
+        for s in range(2):
+            gp = ps_p.tile([P, H], F32, name="gp", tag="p%d" % s)
+            nc.tensor.matmul(out=gp[:], lhsT=ones[:], rhs=zt[:, s, :], start=True, stop=True)
+            nc.scalar.copy(out=gam[:, s * H:(s + 1) * H], in_=gp[:])
+        bs = ps_c.tile([P, H], F32, name="bs")
+        nc.tensor.matmul(out=bs[:], lhsT=ones[:], rhs=zt[:, 2, :], start=True, stop=True)
         for s in range(3):
             nc.vector.quantize_mx(out=wc[:, s, :].bitcast(FP8X4), scales=ws[:, s, :], in_=gw[:, s, :])
 
@@ -142,16 +151,21 @@ def tile_layernormgrucell_pb_t_kernel(tc, x, h, c, W_u, U_u, ln_gamma, ln_beta, 
                 srch = banks[J][2][:].rearrange("p (t u r) -> p t r u", t=2, u=2)
                 nc.scalar.copy(out=ghw.rearrange("p t (r u) -> p t r u", u=2), in_=srch)
 
-        def qz(J):
+        def qzh(J):
+            if not 0 <= J < NT // 2:
+                return
+            chh = cod.tile([P, 256], U32, name="chh", tag="chh", align_bytes=64)
+            shh = cod.tile([P, 256], U8, name="shh", tag="shh", align_bytes=64)
+            nc.vector.quantize_mx(out=chh[:].bitcast(FP8X4), scales=shh[:], in_=gh_t[J][:].rearrange("p t k -> p (t k)"))
+            chh_t[J], shh_t[J] = chh, shh
+
+        def qzx(J):
             if not 0 <= J < NT // 2:
                 return
             cx = cod.tile([P, 512], U32, name="cx", tag="cx", align_bytes=64)
             sx = cod.tile([P, 512], U8, name="sx", tag="sx", align_bytes=64)
-            chh = cod.tile([P, 256], U32, name="chh", tag="chh", align_bytes=64)
-            shh = cod.tile([P, 256], U8, name="shh", tag="shh", align_bytes=64)
-            nc.vector.quantize_mx(out=chh[:].bitcast(FP8X4), scales=shh[:], in_=gh_t[J][:].rearrange("p t k -> p (t k)"))
             nc.vector.quantize_mx(out=cx[:].bitcast(FP8X4), scales=sx[:], in_=gx_t[J][:].rearrange("p t k -> p (t k)"))
-            cx_t[J], sx_t[J], chh_t[J], shh_t[J] = cx, sx, chh, shh
+            cx_t[J], sx_t[J] = cx, sx
 
         def mm(i):
             if not 0 <= i < NT:
@@ -174,8 +188,8 @@ def tile_layernormgrucell_pb_t_kernel(tc, x, h, c, W_u, U_u, ln_gamma, ln_beta, 
                 return
             nm = sml.tile([P, 2], F32, name="nm", tag="nm")
             ss = sml.tile([P, 2], F32, name="ss", tag="ss")
-            q0 = wrk.tile([P, H], F32, name="q0", tag="q0")
-            q1 = wrk.tile([P, H], F32, name="q1", tag="q1")
+            q0 = wrk.tile([P, H], F32, name="q0", tag="q0", bufs=2)
+            q1 = wrk.tile([P, H], F32, name="q1", tag="q1", bufs=2)
             nc.scalar.activation(out=q0[:], in_=p0_t[i][:], func=ACT.Identity, scale=-1.0 / H, accum_out=nm[:, 0:1])
             nc.scalar.activation(out=q1[:], in_=p1_t[i][:], func=ACT.Identity, scale=-1.0 / H, accum_out=nm[:, 1:2])
             nc.scalar.activation(out=q0[:], in_=q0[:], func=ACT.Square, scale=-1.0 * H, bias=nm[:, 0:1], accum_out=ss[:, 0:1])
@@ -202,7 +216,7 @@ def tile_layernormgrucell_pb_t_kernel(tc, x, h, c, W_u, U_u, ln_gamma, ln_beta, 
             if not 0 <= i < NT:
                 return
             a = wrk.tile([P, H], F32, name="a", tag="a")
-            b = wrk.tile([P, H], F32, name="b", tag="b", bufs=4)
+            b = wrk.tile([P, H], F32, name="b", tag="b", bufs=5)
             nc.vector.scalar_tensor_tensor(out=a[:], in0=p0_t[i][:], scalar=nm_t[i][:, 0:1], in1=gam[:, 0:H], op0=ALU.add, op1=ALU.mult)
             nc.vector.scalar_tensor_tensor(out=b[:], in0=p1_t[i][:], scalar=nm_t[i][:, 1:2], in1=gam[:, H:2 * H], op0=ALU.add, op1=ALU.mult)
             a_t[i], b_t[i] = a, b
@@ -234,33 +248,26 @@ def tile_layernormgrucell_pb_t_kernel(tc, x, h, c, W_u, U_u, ln_gamma, ln_beta, 
         if MANUAL:
             ctx.enter_context(tc.manual_schedule())
 
-        tr(0)
-        ev(0, 0)
-        ev(0, 1)
-        tr(1)
-        qz(0)
-        ev(1, 0)
-        ev(1, 1)
-        mm(0)
-        dd(0)
-        dd(1)
-
-        for i in range(NT + 2):
-            if i % CH == 0 and i // CH + 3 < NCH:
+        for i in range(-5, NT + 3):
+            if i >= 0 and i % CH == 0 and i // CH + 3 < NCH:
                 load_h(i // CH + 3)
                 load_x(i // CH + 3)
                 load_c(i // CH + 3)
-            yz(i - 1)
             st(i)
             rs(i)
-            dd(i + 2)
-            sg(i - 1)
-            bl(i - 2)
             ab(i)
-            mm(i + 1)
+            yz(i - 2)
             if i % 2 == 0:
-                tr(i // 2 + 2)
                 ev(i // 2 + 2, 0)
-                qz(i // 2 + 1)
             else:
-                ev((i - 1) // 2 + 2, 1)
+                ev((i + 3) // 2, 1)
+            sg(i - 2)
+            if i % 2 == 0:
+                qzx(i // 2 + 1)
+            else:
+                qzh((i + 3) // 2)
+            bl(i - 3)
+            dd(i + 2)
+            mm(i + 1)
+            if i % 2 != 0:
+                tr((i + 5) // 2)

@@ -15,11 +15,11 @@ ACT = mybir.ActivationFunctionType
 P = 128
 B, IN, H = 4096, 1024, 512
 NT = B // P
+ND = NT // 2
 CH = 4
 NCH = NT // CH
 EPS = 1e-5
 FLOPS = 2 * B * H * (H + IN)
-MANUAL = True
 
 
 def tile_layernormgrucell_pb_t_kernel(tc, x, h, c, W_u, U_u, ln_gamma, ln_beta, out):
@@ -28,16 +28,15 @@ def tile_layernormgrucell_pb_t_kernel(tc, x, h, c, W_u, U_u, ln_gamma, ln_beta, 
         const = ctx.enter_context(tc.tile_pool(name="const", bufs=1))
         xin = ctx.enter_context(tc.tile_pool(name="xin", bufs=4))
         hin = ctx.enter_context(tc.tile_pool(name="hin", bufs=NCH))
-        cin = ctx.enter_context(tc.tile_pool(name="cin", bufs=4))
-        grp = ctx.enter_context(tc.tile_pool(name="grp", bufs=2))
+        cin = ctx.enter_context(tc.tile_pool(name="cin", bufs=5))
+        grp = ctx.enter_context(tc.tile_pool(name="grp", bufs=3))
         cod = ctx.enter_context(tc.tile_pool(name="cod", bufs=3))
         wrk = ctx.enter_context(tc.tile_pool(name="wrk", bufs=4))
-        dpl = ctx.enter_context(tc.tile_pool(name="dpl", bufs=7))
-        sml = ctx.enter_context(tc.tile_pool(name="sml", bufs=5))
+        sml = ctx.enter_context(tc.tile_pool(name="sml", bufs=6))
         opl = ctx.enter_context(tc.tile_pool(name="opl", bufs=3))
-        ps_t = ctx.enter_context(tc.psum_pool(name="ps_t", bufs=1))
-        ps_p = ctx.enter_context(tc.psum_pool(name="ps_p", bufs=2))
-        ps_c = ctx.enter_context(tc.psum_pool(name="ps_c", bufs=1))
+        ps1 = ctx.enter_context(tc.psum_pool(name="ps1", bufs=1))
+        ps3 = ctx.enter_context(tc.psum_pool(name="ps3", bufs=3))
+        ctx.enter_context(tc.manual_schedule())
 
         xv = x.rearrange("(p t) k -> p t k", t=NT)
         hv = h.rearrange("(p t) k -> p t k", t=NT)
@@ -61,14 +60,20 @@ def tile_layernormgrucell_pb_t_kernel(tc, x, h, c, W_u, U_u, ln_gamma, ln_beta, 
             nc.sync.dma_start(out=t[:], in_=cv[:, ci * CH:(ci + 1) * CH, :])
             c_ch[ci] = t
 
-        w_raw = const.tile([P, 4, H], BF16, name="w_raw")
-        nc.sync.dma_start(out=w_raw[:], in_=W_u.rearrange("(b p) k -> p b k", p=P))
-        load_h(0)
-        u_raw = const.tile([P, 4, IN], BF16, name="u_raw")
-        nc.sync.dma_start(out=u_raw[:], in_=U_u.rearrange("(b p) k -> p b k", p=P))
-        load_x(0)
+        def h_of(i):
+            return h_ch[i // CH][:, i % CH, :]
+
+        def c_of(i):
+            return c_ch[i // CH][:, i % CH, :]
+
         zt = const.tile([P, 3, H], BF16, name="zt")
         nc.vector.memset(zt[:].bitcast(I32), 0)
+        w_raw = const.tile([P, 4, H], BF16, name="w_raw")
+        nc.sync.dma_start(out=w_raw[:], in_=W_u.rearrange("(b p) k -> p b k", p=P))
+        u_raw = const.tile([P, 4, IN], BF16, name="u_raw")
+        nc.sync.dma_start(out=u_raw[:], in_=U_u.rearrange("(b p) k -> p b k", p=P))
+        load_h(0)
+        load_x(0)
         nc.sync.dma_start(out=zt[0:1, 0:2, :], in_=ln_gamma.rearrange("(o g) f -> o g f", o=1))
         nc.sync.dma_start(out=zt[0:2, 2, :], in_=ln_beta)
         load_c(0)
@@ -79,21 +84,36 @@ def tile_layernormgrucell_pb_t_kernel(tc, x, h, c, W_u, U_u, ln_gamma, ln_beta, 
 
         ident = const.tile([P, P], F32, name="ident")
         make_identity(nc, ident[:])
-        ones = const.tile([P, P], BF16, name="ones")
-        nc.vector.memset(ones[:], 1.0)
+        identb = const.tile([P, P], BF16, name="identb")
+        make_identity(nc, identb[:])
         mhalf = const.tile([P, 2], F32, name="mhalf")
         nc.gpsimd.memset(mhalf[:], -0.5)
+        ones = const.tile([P, P], BF16, name="ones")
+        nc.vector.memset(ones[:], 1.0)
+        nidentb = const.tile([P, P], BF16, name="nidentb")
+        nc.vector.tensor_scalar(out=nidentb[:], in0=identb[:], scalar1=-1.0, scalar2=None, op0=ALU.mult)
 
         gw = const.tile([P, 3, 4 * H], BF16, name="gw", align_bytes=64)
         wc = const.tile([P, 3, H], U32, name="wc", align_bytes=64)
         ws = const.tile([P, 3, H], U8, name="ws", align_bytes=64)
         gw_w = gw[:].bitcast(F32)
+
+        def quant_w(s):
+            nc.vector.quantize_mx(out=wc[:, s, :].bitcast(FP8X4), scales=ws[:, s, :], in_=gw[:, s, :])
+
         n_bank = 0
         for s in range(3):
             raw_w = (w_raw if s == 0 else u_raw)[:].bitcast(F32)
             g = max(s - 1, 0)
             for j in range(2):
-                bank = ps_t.tile([P, 512], F32, name="xt", tag="xt%d" % (n_bank % 2))
+                if n_bank == 0:
+                    bank = ps1.tile([P, 512], F32, name="wb", tag="xt")
+                elif n_bank == 1:
+                    bank = ps1.tile([P, 512], F32, name="wb", tag="ht")
+                elif n_bank == 5:
+                    bank = ps1.tile([P, 512], F32, name="wb", tag="dd")
+                else:
+                    bank = ps3.tile([P, 512], F32, name="wb", tag="p")
                 for u in range(2):
                     for fl in range(2):
                         nc.tensor.transpose(
@@ -107,94 +127,114 @@ def tile_layernormgrucell_pb_t_kernel(tc, x, h, c, W_u, U_u, ln_gamma, ln_beta, 
                     nc.scalar.copy(out=dst, in_=src)
                 else:
                     nc.vector.tensor_copy(out=dst, in_=src)
+                if n_bank == 3:
+                    quant_w(0)
                 n_bank += 1
-        gam = const.tile([P, 2 * H], F32, name="gam")
-        for s in range(2):
-            gp = ps_p.tile([P, H], F32, name="gp", tag="p%d" % s)
-            nc.tensor.matmul(out=gp[:], lhsT=ones[:], rhs=zt[:, s, :], start=True, stop=True)
-            nc.scalar.copy(out=gam[:, s * H:(s + 1) * H], in_=gp[:])
-        bs = ps_c.tile([P, H], F32, name="bs")
-        nc.tensor.matmul(out=bs[:], lhsT=ones[:], rhs=zt[:, 2, :], start=True, stop=True)
-        for s in range(3):
-            nc.vector.quantize_mx(out=wc[:, s, :].bitcast(FP8X4), scales=ws[:, s, :], in_=gw[:, s, :])
+        quant_w(1)
+        quant_w(2)
 
-        banks, gx_t, gh_t, cx_t, sx_t, chh_t, shh_t = {}, {}, {}, {}, {}, {}, {}
-        p0_t, p1_t, q_t, nm_t, ss_t, r_t, a_t, b_t, d_t, o_t = {}, {}, {}, {}, {}, {}, {}, {}, {}, {}
+        xt_t, ht_t, gx_t, gh_t, cx_t, sx_t, chh_t, shh_t = {}, {}, {}, {}, {}, {}, {}, {}
+        s4_t, p0_t, p1_t, nm_t, ss_t, r_t, a_t, b_t, d_t, o_t = {}, {}, {}, {}, {}, {}, {}, {}, {}, {}
 
-        def tr(J):
-            if not 0 <= J < NT // 2:
+        def on_pe(i):
+            return i % 2 == 0
+
+        def trx(i):
+            if not 0 <= i < NT:
                 return
-            ht = ps_t.tile([P, 512], F32, name="ht", tag="ht")
-            xts = []
+            xw = x_ch[i // CH][:].bitcast(F32)
+            xt = ps1.tile([P, 512], F32, name="xt", tag="xt")
+            for wb in range(4):
+                nc.tensor.transpose(xt[:, wb * P:(wb + 1) * P], xw[:, i % CH, wb * P:(wb + 1) * P], ident[:])
+            xt_t[i] = xt
+
+        def trh(J):
+            if not 0 <= J < ND:
+                return
+            ht = ps1.tile([P, 512], F32, name="ht", tag="ht")
             for tau in range(2):
                 i = 2 * J + tau
-                xw = x_ch[i // CH][:].bitcast(F32)
                 hw = h_ch[i // CH][:].bitcast(F32)
-                xt = ps_t.tile([P, 512], F32, name="xt", tag="xt%d" % tau)
-                for wb in range(4):
-                    nc.tensor.transpose(xt[:, wb * P:(wb + 1) * P], xw[:, i % CH, wb * P:(wb + 1) * P], ident[:])
                 for u in range(2):
                     nc.tensor.transpose(ht[:, (2 * tau + u) * P:(2 * tau + u + 1) * P], hw[:, i % CH, u * P:(u + 1) * P], ident[:])
-                xts.append(xt)
-            banks[J] = (xts[0], xts[1], ht)
-            gx_t[J] = grp.tile([P, 2, IN], BF16, name="gx", tag="gx", align_bytes=64)
-            gh_t[J] = grp.tile([P, 2, H], BF16, name="gh", tag="gh", align_bytes=64)
+            ht_t[J] = ht
 
-        def ev(J, part):
-            if not 0 <= J < NT // 2:
+        def evx(i):
+            if not 0 <= i < NT:
                 return
-            gxw = gx_t[J][:].bitcast(F32)
-            src = banks[J][part][:].rearrange("p (g u r) -> p g r u", g=2, u=2)
-            nc.scalar.copy(out=gxw[:, part, :].rearrange("p (g r u) -> p g r u", g=2, u=2), in_=src)
-            if part == 0:
-                ghw = gh_t[J][:].bitcast(F32)
-                srch = banks[J][2][:].rearrange("p (t u r) -> p t r u", t=2, u=2)
-                nc.scalar.copy(out=ghw.rearrange("p t (r u) -> p t r u", u=2), in_=srch)
+            gx = grp.tile([P, IN], BF16, name="gx", tag="gx", align_bytes=64)
+            nc.scalar.copy(out=gx[:].bitcast(F32).rearrange("p (g r u) -> p g r u", g=2, u=2),
+                           in_=xt_t[i][:].rearrange("p (g u r) -> p g r u", g=2, u=2))
+            gx_t[i] = gx
 
-        def qzh(J):
-            if not 0 <= J < NT // 2:
+        def evh(J):
+            if not 0 <= J < ND:
+                return
+            gh = grp.tile([P, 2 * H], BF16, name="gh", tag="gh", align_bytes=64, bufs=2)
+            nc.scalar.copy(out=gh[:].bitcast(F32).rearrange("p (t r u) -> p t r u", t=2, u=2),
+                           in_=ht_t[J][:].rearrange("p (t u r) -> p t r u", t=2, u=2))
+            gh_t[J] = gh
+
+        def qh(J):
+            if not 0 <= J < ND:
                 return
             chh = cod.tile([P, 256], U32, name="chh", tag="chh", align_bytes=64)
             shh = cod.tile([P, 256], U8, name="shh", tag="shh", align_bytes=64)
-            nc.vector.quantize_mx(out=chh[:].bitcast(FP8X4), scales=shh[:], in_=gh_t[J][:].rearrange("p t k -> p (t k)"))
+            nc.vector.quantize_mx(out=chh[:].bitcast(FP8X4), scales=shh[:], in_=gh_t[J][:])
             chh_t[J], shh_t[J] = chh, shh
 
-        def qzx(J):
-            if not 0 <= J < NT // 2:
+        def qx(i):
+            if not 0 <= i < NT:
                 return
-            cx = cod.tile([P, 512], U32, name="cx", tag="cx", align_bytes=64)
-            sx = cod.tile([P, 512], U8, name="sx", tag="sx", align_bytes=64)
-            nc.vector.quantize_mx(out=cx[:].bitcast(FP8X4), scales=sx[:], in_=gx_t[J][:].rearrange("p t k -> p (t k)"))
-            cx_t[J], sx_t[J] = cx, sx
+            cx = cod.tile([P, 256], U32, name="cx", tag="cx", align_bytes=64)
+            sx = cod.tile([P, 256], U8, name="sx", tag="sx", align_bytes=64)
+            nc.vector.quantize_mx(out=cx[:].bitcast(FP8X4), scales=sx[:], in_=gx_t[i][:])
+            cx_t[i], sx_t[i] = cx, sx
+
+        def mx(dst, lw, ls, s, cols, start, stop):
+            nc.tensor.matmul_mx(out=dst, lhsT=lw.bitcast(FP8X4), lhsT_scale=ls,
+                                rhs=wc[:, s, cols].bitcast(FP8X4), rhs_scale=ws[:, s, cols], start=start, stop=stop)
 
         def mm(i):
             if not 0 <= i < NT:
                 return
             J, tau = i // 2, i % 2
-            p0 = ps_p.tile([P, H], F32, name="p0", tag="p0")
-            p1 = ps_p.tile([P, H], F32, name="p1", tag="p1")
             hs = slice(tau * P, (tau + 1) * P)
-            nc.tensor.matmul_mx(out=p0[:], lhsT=chh_t[J][:, hs].bitcast(FP8X4), lhsT_scale=shh_t[J][:, hs],
-                                rhs=wc[:, 0, :].bitcast(FP8X4), rhs_scale=ws[:, 0, :], start=True, stop=True)
+            hw_, hsc = chh_t[J][:, hs], shh_t[J][:, hs]
+            xw_ = [cx_t[i][:, g * P:(g + 1) * P] for g in range(2)]
+            xsc = [sx_t[i][:, g * P:(g + 1) * P] for g in range(2)]
+            s4 = ps1.tile([P, 2 * P], F32, name="s4", tag="s4")
+            for fb in range(4):
+                mx(s4[:, 0:P], hw_, hsc, 0, slice(fb * P, (fb + 1) * P), fb == 0, fb == 3)
             for g in range(2):
-                xs = slice(tau * 256 + g * P, tau * 256 + (g + 1) * P)
-                nc.tensor.matmul_mx(out=p1[:], lhsT=cx_t[J][:, xs].bitcast(FP8X4), lhsT_scale=sx_t[J][:, xs],
-                                    rhs=wc[:, 1 + g, :].bitcast(FP8X4), rhs_scale=ws[:, 1 + g, :],
-                                    start=(g == 0), stop=(g == 1))
-            p0_t[i], p1_t[i] = p0, p1
+                for fb in range(4):
+                    mx(s4[:, P:2 * P], xw_[g], xsc[g], 1 + g, slice(fb * P, (fb + 1) * P), g == 0 and fb == 0, g == 1 and fb == 3)
+            p0 = ps3.tile([P, H], F32, name="p0", tag="p")
+            mx(p0[:], hw_, hsc, 0, slice(0, H), True, True)
+            p1 = ps3.tile([P, H], F32, name="p1", tag="p")
+            for g in range(2):
+                mx(p1[:], xw_[g], xsc[g], 1 + g, slice(0, H), g == 0, g == 1)
+            s4_t[i], p0_t[i], p1_t[i] = s4, p0, p1
 
-        def st(i):
+        def mean(i):
             if not 0 <= i < NT:
                 return
             nm = sml.tile([P, 2], F32, name="nm", tag="nm")
+            mj = wrk.tile([P, 2 * P], F32, name="mj", tag="mj", bufs=2)
+            for l in range(2):
+                nc.scalar.activation(out=mj[:, l * P:(l + 1) * P], in_=s4_t[i][:, l * P:(l + 1) * P], func=ACT.Identity,
+                                     scale=-1.0 / H, accum_out=nm[:, l:l + 1])
+            nm_t[i] = nm
+
+        def sq(i):
+            if not 0 <= i < NT:
+                return
             ss = sml.tile([P, 2], F32, name="ss", tag="ss")
-            q0 = wrk.tile([P, H], F32, name="q0", tag="q0", bufs=2)
-            q1 = wrk.tile([P, H], F32, name="q1", tag="q1", bufs=2)
-            nc.scalar.activation(out=q0[:], in_=p0_t[i][:], func=ACT.Identity, scale=-1.0 / H, accum_out=nm[:, 0:1])
-            nc.scalar.activation(out=q1[:], in_=p1_t[i][:], func=ACT.Identity, scale=-1.0 / H, accum_out=nm[:, 1:2])
-            nc.scalar.activation(out=q0[:], in_=q0[:], func=ACT.Square, scale=-1.0 * H, bias=nm[:, 0:1], accum_out=ss[:, 0:1])
-            nc.scalar.activation(out=q1[:], in_=q1[:], func=ACT.Square, scale=-1.0 * H, bias=nm[:, 1:2], accum_out=ss[:, 1:2])
-            nm_t[i], ss_t[i] = nm, ss
+            a = wrk.tile([P, H], F32, name="a", tag="a")
+            b = wrk.tile([P, H], F32, name="b", tag="b", bufs=6)
+            nc.scalar.activation(out=a[:], in_=p0_t[i][:], func=ACT.Square, bias=nm_t[i][:, 0:1], accum_out=ss[:, 0:1])
+            nc.scalar.activation(out=b[:], in_=p1_t[i][:], func=ACT.Square, bias=nm_t[i][:, 1:2], accum_out=ss[:, 1:2])
+            ss_t[i], a_t[i], b_t[i] = ss, a, b
 
         def rs(i):
             if not 0 <= i < NT:
@@ -205,21 +245,26 @@ def tile_layernormgrucell_pb_t_kernel(tc, x, h, c, W_u, U_u, ln_gamma, ln_beta, 
             nc.gpsimd.tensor_tensor(out=r[:], in0=v[:], in1=mhalf[:], op=ALU.pow)
             r_t[i] = r
 
-        def dd(i):
-            if not 0 <= i < NT:
+        def d_g(i):
+            if not 0 <= i < NT or on_pe(i):
                 return
-            dt_ = dpl.tile([P, H], F32, name="d", tag="d")
-            nc.gpsimd.tensor_tensor(out=dt_[:], in0=c_ch[i // CH][:, i % CH, :], in1=h_ch[i // CH][:, i % CH, :], op=ALU.subtract)
+            dt_ = wrk.tile([P, H], F32, name="d", tag="d")
+            nc.gpsimd.tensor_tensor(out=dt_[:], in0=c_of(i), in1=h_of(i), op=ALU.subtract)
             d_t[i] = dt_
+
+        def d_p(i):
+            if not 0 <= i < NT or not on_pe(i):
+                return
+            dp = ps1.tile([P, H], F32, name="dp", tag="dd")
+            nc.tensor.matmul(out=dp[:], lhsT=identb[:], rhs=c_of(i), start=True, stop=False)
+            nc.tensor.matmul(out=dp[:], lhsT=nidentb[:], rhs=h_of(i), start=False, stop=True)
+            d_t[i] = dp
 
         def ab(i):
             if not 0 <= i < NT:
                 return
-            a = wrk.tile([P, H], F32, name="a", tag="a")
-            b = wrk.tile([P, H], F32, name="b", tag="b", bufs=5)
-            nc.vector.scalar_tensor_tensor(out=a[:], in0=p0_t[i][:], scalar=nm_t[i][:, 0:1], in1=gam[:, 0:H], op0=ALU.add, op1=ALU.mult)
-            nc.vector.scalar_tensor_tensor(out=b[:], in0=p1_t[i][:], scalar=nm_t[i][:, 1:2], in1=gam[:, H:2 * H], op0=ALU.add, op1=ALU.mult)
-            a_t[i], b_t[i] = a, b
+            nc.vector.scalar_tensor_tensor(out=a_t[i][:], in0=p0_t[i][:], scalar=nm_t[i][:, 0:1], in1=gam[:, 0:H], op0=ALU.add, op1=ALU.mult)
+            nc.vector.scalar_tensor_tensor(out=b_t[i][:], in0=p1_t[i][:], scalar=nm_t[i][:, 1:2], in1=gam[:, H:2 * H], op0=ALU.add, op1=ALU.mult)
 
         def yz(i):
             if not 0 <= i < NT:
@@ -241,33 +286,61 @@ def tile_layernormgrucell_pb_t_kernel(tc, x, h, c, W_u, U_u, ln_gamma, ln_beta, 
                 o_t[J] = opl.tile([P, 2, H], F32, name="o", tag="o")
             o = o_t[J]
             nc.vector.tensor_tensor(out=o[:, tau, :], in0=b_t[i][:], in1=d_t[i][:], op=ALU.mult)
-            nc.vector.tensor_tensor(out=o[:, tau, :], in0=o[:, tau, :], in1=h_ch[i // CH][:, i % CH, :], op=ALU.add)
-            if tau == 1:
-                nc.sync.dma_start(out=ov[:, 2 * J:2 * J + 2, :], in_=o[:])
+            if on_pe(i):
+                nc.gpsimd.tensor_tensor(out=o[:, tau, :], in0=o[:, tau, :], in1=h_of(i), op=ALU.add)
+            else:
+                nc.vector.tensor_tensor(out=o[:, tau, :], in0=o[:, tau, :], in1=h_of(i), op=ALU.add)
 
-        if MANUAL:
-            ctx.enter_context(tc.manual_schedule())
+        def store(J):
+            if not 0 <= J < ND:
+                return
+            nc.sync.dma_start(out=ov[:, 2 * J:2 * J + 2, :], in_=o_t[J][:])
 
-        for i in range(-5, NT + 3):
-            if i >= 0 and i % CH == 0 and i // CH + 3 < NCH:
+        trh(0)
+        trx(0)
+        gam = const.tile([P, 2 * H], F32, name="gam")
+        for s in range(2):
+            gp = ps3.tile([P, H], F32, name="gp", tag="p")
+            nc.tensor.matmul(out=gp[:], lhsT=ones[:], rhs=zt[:, s, :], start=True, stop=True)
+            nc.vector.tensor_copy(out=gam[:, s * H:(s + 1) * H], in_=gp[:])
+        bs = ps1.tile([P, H], F32, name="bs", tag="bs")
+        nc.tensor.matmul(out=bs[:], lhsT=ones[:], rhs=zt[:, 2, :], start=True, stop=True)
+        evh(0)
+        evx(0)
+        trx(1)
+        qh(0)
+        qx(0)
+        mm(0)
+        evx(1)
+        trx(2)
+        trh(1)
+        qx(1)
+        d_g(1)
+
+        for i in range(NT + 5):
+            even = i % 2 == 0
+            if i % CH == 0 and i // CH + 3 < NCH:
                 load_h(i // CH + 3)
                 load_x(i // CH + 3)
                 load_c(i // CH + 3)
-            st(i)
+            mean(i)
+            sq(i)
             rs(i)
             ab(i)
             yz(i - 2)
-            if i % 2 == 0:
-                ev(i // 2 + 2, 0)
-            else:
-                ev((i + 3) // 2, 1)
-            sg(i - 2)
-            if i % 2 == 0:
-                qzx(i // 2 + 1)
-            else:
-                qzh((i + 3) // 2)
-            bl(i - 3)
-            dd(i + 2)
+            evx(i + 2)
+            if even:
+                evh(i // 2 + 1)
+            sg(i - 3)
+            qx(i + 2)
+            if even:
+                qh(i // 2 + 1)
+            bl(i - 4)
+            d_g(i + 2)
+            if not even:
+                store((i - 5) // 2)
             mm(i + 1)
-            if i % 2 != 0:
-                tr((i + 5) // 2)
+            trx(i + 3)
+            if not even:
+                trh((i + 3) // 2)
+            d_p(i - 2)

@@ -33,7 +33,7 @@ def tile_layernormgrucell_pb_t_kernel(tc, x, h, c, W_u, U_u, ln_gamma, ln_beta, 
         cod = ctx.enter_context(tc.tile_pool(name="cod", bufs=3))
         wrk = ctx.enter_context(tc.tile_pool(name="wrk", bufs=4))
         sml = ctx.enter_context(tc.tile_pool(name="sml", bufs=6))
-        opl = ctx.enter_context(tc.tile_pool(name="opl", bufs=3))
+        opl = ctx.enter_context(tc.tile_pool(name="opl", bufs=4))
         ps1 = ctx.enter_context(tc.psum_pool(name="ps1", bufs=1))
         ps3 = ctx.enter_context(tc.psum_pool(name="ps3", bufs=3))
         ctx.enter_context(tc.manual_schedule())
@@ -68,12 +68,16 @@ def tile_layernormgrucell_pb_t_kernel(tc, x, h, c, W_u, U_u, ln_gamma, ln_beta, 
 
         zt = const.tile([P, 3, H], BF16, name="zt")
         nc.vector.memset(zt[:].bitcast(I32), 0)
-        w_raw = const.tile([P, 4, H], BF16, name="w_raw")
-        nc.sync.dma_start(out=w_raw[:], in_=W_u.rearrange("(b p) k -> p b k", p=P))
+        h_ch[0] = hin.tile([P, CH, H], BF16, name="h_ch", tag="h_ch")
+        x_ch[0] = xin.tile([P, CH, IN], BF16, name="x_ch", tag="x_ch")
+        nc.sync.dma_start(out=h_ch[0][:, 0:2, :], in_=hv[:, 0:2, :])
+        nc.sync.dma_start(out=x_ch[0][:, 0:2, :], in_=xv[:, 0:2, :])
         u_raw = const.tile([P, 4, IN], BF16, name="u_raw")
         nc.sync.dma_start(out=u_raw[:], in_=U_u.rearrange("(b p) k -> p b k", p=P))
-        load_h(0)
-        load_x(0)
+        w_raw = const.tile([P, 4, H], BF16, name="w_raw")
+        nc.sync.dma_start(out=w_raw[:], in_=W_u.rearrange("(b p) k -> p b k", p=P))
+        nc.sync.dma_start(out=h_ch[0][:, 2:4, :], in_=hv[:, 2:4, :])
+        nc.sync.dma_start(out=x_ch[0][:, 2:4, :], in_=xv[:, 2:4, :])
         nc.sync.dma_start(out=zt[0:1, 0:2, :], in_=ln_gamma.rearrange("(o g) f -> o g f", o=1))
         nc.sync.dma_start(out=zt[0:2, 2, :], in_=ln_beta)
         load_c(0)
@@ -101,37 +105,22 @@ def tile_layernormgrucell_pb_t_kernel(tc, x, h, c, W_u, U_u, ln_gamma, ln_beta, 
         def quant_w(s):
             nc.vector.quantize_mx(out=wc[:, s, :].bitcast(FP8X4), scales=ws[:, s, :], in_=gw[:, s, :])
 
-        n_bank = 0
-        for s in range(3):
+        def prep_w(s, j, bank, on_scalar):
             raw_w = (w_raw if s == 0 else u_raw)[:].bitcast(F32)
             g = max(s - 1, 0)
-            for j in range(2):
-                if n_bank == 0:
-                    bank = ps1.tile([P, 512], F32, name="wb", tag="xt")
-                elif n_bank == 1:
-                    bank = ps1.tile([P, 512], F32, name="wb", tag="ht")
-                elif n_bank == 5:
-                    bank = ps1.tile([P, 512], F32, name="wb", tag="dd")
-                else:
-                    bank = ps3.tile([P, 512], F32, name="wb", tag="p")
-                for u in range(2):
-                    for fl in range(2):
-                        nc.tensor.transpose(
-                            bank[:, u * 256 + fl * P:u * 256 + (fl + 1) * P],
-                            raw_w[:, 2 * j + fl, (2 * g + u) * P:(2 * g + u + 1) * P],
-                            ident[:],
-                        )
-                dst = gw_w[:, s, j * 512:(j + 1) * 512].rearrange("p (f u) -> p f u", u=2)
-                src = bank[:].rearrange("p (u f) -> p f u", u=2)
-                if n_bank % 2 == 0:
-                    nc.scalar.copy(out=dst, in_=src)
-                else:
-                    nc.vector.tensor_copy(out=dst, in_=src)
-                if n_bank == 3:
-                    quant_w(0)
-                n_bank += 1
-        quant_w(1)
-        quant_w(2)
+            for u in range(2):
+                for fl in range(2):
+                    nc.tensor.transpose(
+                        bank[:, u * 256 + fl * P:u * 256 + (fl + 1) * P],
+                        raw_w[:, 2 * j + fl, (2 * g + u) * P:(2 * g + u + 1) * P],
+                        ident[:],
+                    )
+            dst = gw_w[:, s, j * 512:(j + 1) * 512].rearrange("p (f u) -> p f u", u=2)
+            src = bank[:].rearrange("p (u f) -> p f u", u=2)
+            if on_scalar:
+                nc.scalar.copy(out=dst, in_=src)
+            else:
+                nc.vector.tensor_copy(out=dst, in_=src)
 
         xt_t, ht_t, gx_t, gh_t, cx_t, sx_t, chh_t, shh_t = {}, {}, {}, {}, {}, {}, {}, {}
         s4_t, p0_t, p1_t, nm_t, ss_t, r_t, a_t, b_t, d_t, o_t = {}, {}, {}, {}, {}, {}, {}, {}, {}, {}
@@ -286,30 +275,47 @@ def tile_layernormgrucell_pb_t_kernel(tc, x, h, c, W_u, U_u, ln_gamma, ln_beta, 
                 o_t[J] = opl.tile([P, 2, H], F32, name="o", tag="o")
             o = o_t[J]
             nc.vector.tensor_tensor(out=o[:, tau, :], in0=b_t[i][:], in1=d_t[i][:], op=ALU.mult)
-            if on_pe(i):
-                nc.gpsimd.tensor_tensor(out=o[:, tau, :], in0=o[:, tau, :], in1=h_of(i), op=ALU.add)
-            else:
+            if i == NT - 1:
                 nc.vector.tensor_tensor(out=o[:, tau, :], in0=o[:, tau, :], in1=h_of(i), op=ALU.add)
+                nc.sync.dma_start(out=ov[:, i, :], in_=o[:, tau, :])
 
-        def store(J):
-            if not 0 <= J < ND:
+        def add_h(i):
+            if not 0 <= i < NT - 1:
                 return
-            nc.sync.dma_start(out=ov[:, 2 * J:2 * J + 2, :], in_=o_t[J][:])
+            J, tau = i // 2, i % 2
+            o = o_t[J]
+            nc.gpsimd.tensor_tensor(out=o[:, tau, :], in0=o[:, tau, :], in1=h_of(i), op=ALU.add)
+            if i == NT - 2:
+                nc.sync.dma_start(out=ov[:, i, :], in_=o[:, tau, :])
+            elif tau == 1:
+                nc.sync.dma_start(out=ov[:, 2 * J:2 * J + 2, :], in_=o[:])
 
         trh(0)
         trx(0)
+        evh(0)
+        evx(0)
+        qh(0)
+        qx(0)
+        prep_w(1, 0, ps3.tile([P, 512], F32, name="wb0", tag="p"), True)
+        prep_w(1, 1, ps3.tile([P, 512], F32, name="wb1", tag="p"), False)
+        prep_w(2, 0, ps3.tile([P, 512], F32, name="wb2", tag="p"), True)
+        prep_w(2, 1, ps1.tile([P, 512], F32, name="wb3", tag="dd"), False)
+        quant_w(1)
+        prep_w(0, 0, ps1.tile([P, 512], F32, name="wb4", tag="s4"), True)
+        prep_w(0, 1, ps1.tile([P, 512], F32, name="wb5", tag="ht"), False)
+        quant_w(2)
+        trx(1)
         gam = const.tile([P, 2 * H], F32, name="gam")
         for s in range(2):
             gp = ps3.tile([P, H], F32, name="gp", tag="p")
             nc.tensor.matmul(out=gp[:], lhsT=ones[:], rhs=zt[:, s, :], start=True, stop=True)
-            nc.vector.tensor_copy(out=gam[:, s * H:(s + 1) * H], in_=gp[:])
+            if s == 0:
+                nc.vector.tensor_copy(out=gam[:, s * H:(s + 1) * H], in_=gp[:])
+                quant_w(0)
+            else:
+                nc.vector.tensor_copy(out=gam[:, s * H:(s + 1) * H], in_=gp[:])
         bs = ps1.tile([P, H], F32, name="bs", tag="bs")
         nc.tensor.matmul(out=bs[:], lhsT=ones[:], rhs=zt[:, 2, :], start=True, stop=True)
-        evh(0)
-        evx(0)
-        trx(1)
-        qh(0)
-        qx(0)
         mm(0)
         evx(1)
         trx(2)
@@ -317,15 +323,17 @@ def tile_layernormgrucell_pb_t_kernel(tc, x, h, c, W_u, U_u, ln_gamma, ln_beta, 
         qx(1)
         d_g(1)
 
-        for i in range(NT + 5):
+        for i in range(NT + 6):
             even = i % 2 == 0
             if i % CH == 0 and i // CH + 3 < NCH:
                 load_h(i // CH + 3)
                 load_x(i // CH + 3)
                 load_c(i // CH + 3)
+            d_p(i - 4)
             mean(i)
             sq(i)
             rs(i)
+            add_h(i - 5)
             ab(i)
             yz(i - 2)
             evx(i + 2)
@@ -337,10 +345,7 @@ def tile_layernormgrucell_pb_t_kernel(tc, x, h, c, W_u, U_u, ln_gamma, ln_beta, 
                 qh(i // 2 + 1)
             bl(i - 4)
             d_g(i + 2)
-            if not even:
-                store((i - 5) // 2)
             mm(i + 1)
             trx(i + 3)
             if not even:
                 trh((i + 3) // 2)
-            d_p(i - 2)

@@ -33,7 +33,7 @@ def tile_layernormgrucell_pb_t_kernel(tc, x, h, c, W_u, U_u, ln_gamma, ln_beta, 
         cod = ctx.enter_context(tc.tile_pool(name="cod", bufs=3))
         wrk = ctx.enter_context(tc.tile_pool(name="wrk", bufs=4))
         sml = ctx.enter_context(tc.tile_pool(name="sml", bufs=6))
-        opl = ctx.enter_context(tc.tile_pool(name="opl", bufs=4))
+        opl = ctx.enter_context(tc.tile_pool(name="opl", bufs=3))
         ps1 = ctx.enter_context(tc.psum_pool(name="ps1", bufs=1))
         ps3 = ctx.enter_context(tc.psum_pool(name="ps3", bufs=3))
         ctx.enter_context(tc.manual_schedule())
@@ -237,7 +237,7 @@ def tile_layernormgrucell_pb_t_kernel(tc, x, h, c, W_u, U_u, ln_gamma, ln_beta, 
         def d_g(i):
             if not 0 <= i < NT or on_pe(i):
                 return
-            dt_ = wrk.tile([P, H], F32, name="d", tag="d")
+            dt_ = wrk.tile([P, H], F32, name="d", tag="d", bufs=3)
             nc.gpsimd.tensor_tensor(out=dt_[:], in0=c_of(i), in1=h_of(i), op=ALU.subtract)
             d_t[i] = dt_
 
@@ -249,46 +249,51 @@ def tile_layernormgrucell_pb_t_kernel(tc, x, h, c, W_u, U_u, ln_gamma, ln_beta, 
             nc.tensor.matmul(out=dp[:], lhsT=nidentb[:], rhs=h_of(i), start=False, stop=True)
             d_t[i] = dp
 
-        def ab(i):
-            if not 0 <= i < NT:
-                return
-            nc.vector.scalar_tensor_tensor(out=a_t[i][:], in0=p0_t[i][:], scalar=nm_t[i][:, 0:1], in1=gam[:, 0:H], op0=ALU.add, op1=ALU.mult)
-            nc.vector.scalar_tensor_tensor(out=b_t[i][:], in0=p1_t[i][:], scalar=nm_t[i][:, 1:2], in1=gam[:, H:2 * H], op0=ALU.add, op1=ALU.mult)
+        def op_a(i):
+            if 0 <= i < NT:
+                nc.vector.scalar_tensor_tensor(out=a_t[i][:], in0=p0_t[i][:], scalar=nm_t[i][:, 0:1], in1=gam[:, 0:H], op0=ALU.add, op1=ALU.mult)
 
-        def yz(i):
-            if not 0 <= i < NT:
-                return
-            a, b, r = a_t[i], b_t[i], r_t[i]
-            nc.vector.scalar_tensor_tensor(out=a[:], in0=a[:], scalar=r[:, 0:1], in1=bs[:], op0=ALU.mult, op1=ALU.add)
-            nc.vector.scalar_tensor_tensor(out=b[:], in0=b[:], scalar=r[:, 1:2], in1=a[:], op0=ALU.mult, op1=ALU.add)
+        def op_b(i):
+            if 0 <= i < NT:
+                nc.vector.scalar_tensor_tensor(out=b_t[i][:], in0=p1_t[i][:], scalar=nm_t[i][:, 1:2], in1=gam[:, H:2 * H], op0=ALU.add, op1=ALU.mult)
+
+        def op_y(i):
+            if 0 <= i < NT:
+                nc.vector.scalar_tensor_tensor(out=a_t[i][:], in0=a_t[i][:], scalar=r_t[i][:, 0:1], in1=bs[:], op0=ALU.mult, op1=ALU.add)
+
+        def op_z(i):
+            if 0 <= i < NT:
+                nc.vector.scalar_tensor_tensor(out=b_t[i][:], in0=b_t[i][:], scalar=r_t[i][:, 1:2], in1=a_t[i][:], op0=ALU.mult, op1=ALU.add)
 
         def sg(i):
             if not 0 <= i < NT:
                 return
             nc.scalar.activation(out=b_t[i][:], in_=b_t[i][:], func=ACT.Sigmoid)
 
-        def bl(i):
+        def op_e(i):
             if not 0 <= i < NT:
                 return
             J, tau = i // 2, i % 2
             if tau == 0:
                 o_t[J] = opl.tile([P, 2, H], F32, name="o", tag="o")
-            o = o_t[J]
-            nc.vector.tensor_tensor(out=o[:, tau, :], in0=b_t[i][:], in1=d_t[i][:], op=ALU.mult)
-            if i == NT - 1:
-                nc.vector.tensor_tensor(out=o[:, tau, :], in0=o[:, tau, :], in1=h_of(i), op=ALU.add)
-                nc.sync.dma_start(out=ov[:, i, :], in_=o[:, tau, :])
+            nc.vector.tensor_tensor(out=o_t[J][:, tau, :], in0=b_t[i][:], in1=d_t[i][:], op=ALU.mult)
 
-        def add_h(i):
-            if not 0 <= i < NT - 1:
+        def op_o(i):
+            if not 0 <= i < NT:
                 return
             J, tau = i // 2, i % 2
             o = o_t[J]
-            nc.gpsimd.tensor_tensor(out=o[:, tau, :], in0=o[:, tau, :], in1=h_of(i), op=ALU.add)
-            if i == NT - 2:
+            if (on_pe(i) and i != NT - 2) or i == NT - 3:
+                nc.gpsimd.tensor_tensor(out=o[:, tau, :], in0=o[:, tau, :], in1=h_of(i), op=ALU.add)
+            else:
+                nc.vector.tensor_tensor(out=o[:, tau, :], in0=o[:, tau, :], in1=h_of(i), op=ALU.add)
+            if J == ND - 1:
                 nc.sync.dma_start(out=ov[:, i, :], in_=o[:, tau, :])
-            elif tau == 1:
-                nc.sync.dma_start(out=ov[:, 2 * J:2 * J + 2, :], in_=o[:])
+
+        def store(J):
+            if not 0 <= J < ND - 1:
+                return
+            nc.sync.dma_start(out=ov[:, 2 * J:2 * J + 2, :], in_=o_t[J][:])
 
         trh(0)
         trx(0)
@@ -323,7 +328,7 @@ def tile_layernormgrucell_pb_t_kernel(tc, x, h, c, W_u, U_u, ln_gamma, ln_beta, 
         qx(1)
         d_g(1)
 
-        for i in range(NT + 6):
+        for i in range(NT + 5):
             even = i % 2 == 0
             if i % CH == 0 and i // CH + 3 < NCH:
                 load_h(i // CH + 3)
@@ -333,18 +338,22 @@ def tile_layernormgrucell_pb_t_kernel(tc, x, h, c, W_u, U_u, ln_gamma, ln_beta, 
             mean(i)
             sq(i)
             rs(i)
-            add_h(i - 5)
-            ab(i)
-            yz(i - 2)
+            op_a(i)
+            op_y(i - 2)
+            op_b(i)
+            op_z(i - 2)
             evx(i + 2)
             if even:
                 evh(i // 2 + 1)
             sg(i - 3)
+            op_e(i - 4)
             qx(i + 2)
             if even:
                 qh(i // 2 + 1)
-            bl(i - 4)
+            op_o(i - 4)
             d_g(i + 2)
+            if not even:
+                store((i - 5) // 2)
             mm(i + 1)
             trx(i + 3)
             if not even:

@@ -92,6 +92,8 @@ def tile_layernormgrucell_pb_t_kernel(tc, x, h, c, W_u, U_u, ln_gamma, ln_beta, 
         make_identity(nc, identb[:])
         mhalf = const.tile([P, 2], F32, name="mhalf")
         nc.gpsimd.memset(mhalf[:], -0.5)
+        epst = const.tile([P, 1], F32, name="epst")
+        nc.gpsimd.memset(epst[:], EPS)
         ones = const.tile([P, P], BF16, name="ones")
         nc.vector.memset(ones[:], 1.0)
         nidentb = const.tile([P, P], BF16, name="nidentb")
@@ -230,7 +232,7 @@ def tile_layernormgrucell_pb_t_kernel(tc, x, h, c, W_u, U_u, ln_gamma, ln_beta, 
                 return
             v = sml.tile([P, 2], F32, name="v", tag="v")
             r = sml.tile([P, 2], F32, name="r", tag="r")
-            nc.gpsimd.tensor_scalar(out=v[:], in0=ss_t[i][:], scalar1=1.0 / H, scalar2=EPS, op0=ALU.mult, op1=ALU.add)
+            nc.scalar.activation(out=v[:], in_=ss_t[i][:], func=ACT.Identity, scale=1.0 / H, bias=epst[:, 0:1])
             nc.gpsimd.tensor_tensor(out=r[:], in0=v[:], in1=mhalf[:], op=ALU.pow)
             r_t[i] = r
 

@@ -13,350 +13,309 @@ ALU = mybir.AluOpType
 ACT = mybir.ActivationFunctionType
 
 P = 128
-B, IN, H = 4096, 1024, 512
-NT = B // P
-ND = NT // 2
-CH = 4
-NCH = NT // CH
+ROWS, IN, H = 4096, 1024, 512
+BANK = 512
+TILES = ROWS // P
+PAIRS = TILES // 2
+CHUNK = 4
+CHUNKS = TILES // CHUNK
+AHEAD = 3
 EPS = 1e-5
-FLOPS = 2 * B * H * (H + IN)
+FLOPS = 2 * ROWS * H * (H + IN)
 
 
 def tile_layernormgrucell_pb_t_kernel(tc, x, h, c, W_u, U_u, ln_gamma, ln_beta, out):
     nc = tc.nc
     with ExitStack() as ctx:
         const = ctx.enter_context(tc.tile_pool(name="const", bufs=1))
-        xin = ctx.enter_context(tc.tile_pool(name="xin", bufs=4))
-        hin = ctx.enter_context(tc.tile_pool(name="hin", bufs=NCH))
-        cin = ctx.enter_context(tc.tile_pool(name="cin", bufs=5))
-        grp = ctx.enter_context(tc.tile_pool(name="grp", bufs=3))
-        cod = ctx.enter_context(tc.tile_pool(name="cod", bufs=3))
-        wrk = ctx.enter_context(tc.tile_pool(name="wrk", bufs=4))
-        sml = ctx.enter_context(tc.tile_pool(name="sml", bufs=6))
-        opl = ctx.enter_context(tc.tile_pool(name="opl", bufs=3))
-        ps1 = ctx.enter_context(tc.psum_pool(name="ps1", bufs=1))
-        ps3 = ctx.enter_context(tc.psum_pool(name="ps3", bufs=3))
+        x_pool = ctx.enter_context(tc.tile_pool(name="x_pool", bufs=AHEAD + 1))
+        h_pool = ctx.enter_context(tc.tile_pool(name="h_pool", bufs=CHUNKS))
+        c_pool = ctx.enter_context(tc.tile_pool(name="c_pool", bufs=AHEAD + 2))
+        front = ctx.enter_context(tc.tile_pool(name="front", bufs=3))
+        work = ctx.enter_context(tc.tile_pool(name="work", bufs=4))
+        stats = ctx.enter_context(tc.tile_pool(name="stats", bufs=6))
+        psum_ring = ctx.enter_context(tc.psum_pool(name="psum_ring", bufs=3))
+        psum_one = ctx.enter_context(tc.psum_pool(name="psum_one", bufs=1))
         ctx.enter_context(tc.manual_schedule())
 
-        xv = x.rearrange("(p t) k -> p t k", t=NT)
-        hv = h.rearrange("(p t) k -> p t k", t=NT)
-        cv = c.rearrange("(p t) k -> p t k", t=NT)
-        ov = out.rearrange("(p t) f -> p t f", t=NT)
+        x_rows = x.rearrange("(p t) k -> p t k", t=TILES)
+        h_rows = h.rearrange("(p t) k -> p t k", t=TILES)
+        c_rows = c.rearrange("(p t) k -> p t k", t=TILES)
+        out_rows = out.rearrange("(p t) f -> p t f", t=TILES)
 
-        x_ch, h_ch, c_ch = {}, {}, {}
+        x_chunk, h_chunk, c_chunk = {}, {}, {}
 
-        def load_h(ci):
-            t = hin.tile([P, CH, H], BF16, name="h_ch", tag="h_ch")
-            nc.sync.dma_start(out=t[:], in_=hv[:, ci * CH:(ci + 1) * CH, :])
-            h_ch[ci] = t
+        def load(pool, chunks, rows, width, n, first=0, last=CHUNK):
+            if first == 0:
+                chunks[n] = pool.tile([P, CHUNK, width], BF16, name="chunk", tag="chunk")
+            nc.sync.dma_start(out=chunks[n][:, first:last, :], in_=rows[:, n * CHUNK + first:n * CHUNK + last, :])
 
-        def load_x(ci):
-            t = xin.tile([P, CH, IN], BF16, name="x_ch", tag="x_ch")
-            nc.sync.dma_start(out=t[:], in_=xv[:, ci * CH:(ci + 1) * CH, :])
-            x_ch[ci] = t
+        def load_chunk(n):
+            load(h_pool, h_chunk, h_rows, H, n)
+            load(x_pool, x_chunk, x_rows, IN, n)
+            load(c_pool, c_chunk, c_rows, H, n)
 
-        def load_c(ci):
-            t = cin.tile([P, CH, H], BF16, name="c_ch", tag="c_ch")
-            nc.sync.dma_start(out=t[:], in_=cv[:, ci * CH:(ci + 1) * CH, :])
-            c_ch[ci] = t
+        def h_of(t):
+            return h_chunk[t // CHUNK][:, t % CHUNK, :]
 
-        def h_of(i):
-            return h_ch[i // CH][:, i % CH, :]
+        def c_of(t):
+            return c_chunk[t // CHUNK][:, t % CHUNK, :]
 
-        def c_of(i):
-            return c_ch[i // CH][:, i % CH, :]
-
-        zt = const.tile([P, 3, H], BF16, name="zt")
-        nc.vector.memset(zt[:].bitcast(I32), 0)
-        h_ch[0] = hin.tile([P, CH, H], BF16, name="h_ch", tag="h_ch")
-        x_ch[0] = xin.tile([P, CH, IN], BF16, name="x_ch", tag="x_ch")
-        nc.sync.dma_start(out=h_ch[0][:, 0:2, :], in_=hv[:, 0:2, :])
-        nc.sync.dma_start(out=x_ch[0][:, 0:2, :], in_=xv[:, 0:2, :])
+        vectors = const.tile([P, 3, H], BF16, name="vectors")
+        nc.vector.memset(vectors[:].bitcast(I32), 0)
+        load(h_pool, h_chunk, h_rows, H, 0, 0, 2)
+        load(x_pool, x_chunk, x_rows, IN, 0, 0, 2)
+        nc.sync.dma_start(out=vectors[0:1, 0:2, :], in_=ln_gamma.rearrange("(o g) f -> o g f", o=1))
+        nc.sync.dma_start(out=vectors[0:2, 2, :], in_=ln_beta)
         u_raw = const.tile([P, 4, IN], BF16, name="u_raw")
         nc.sync.dma_start(out=u_raw[:], in_=U_u.rearrange("(b p) k -> p b k", p=P))
         w_raw = const.tile([P, 4, H], BF16, name="w_raw")
         nc.sync.dma_start(out=w_raw[:], in_=W_u.rearrange("(b p) k -> p b k", p=P))
-        nc.sync.dma_start(out=h_ch[0][:, 2:4, :], in_=hv[:, 2:4, :])
-        nc.sync.dma_start(out=x_ch[0][:, 2:4, :], in_=xv[:, 2:4, :])
-        nc.sync.dma_start(out=zt[0:1, 0:2, :], in_=ln_gamma.rearrange("(o g) f -> o g f", o=1))
-        nc.sync.dma_start(out=zt[0:2, 2, :], in_=ln_beta)
-        load_c(0)
-        for ci in (1, 2):
-            load_h(ci)
-            load_x(ci)
-            load_c(ci)
+        load(h_pool, h_chunk, h_rows, H, 0, 2, CHUNK)
+        load(x_pool, x_chunk, x_rows, IN, 0, 2, CHUNK)
+        load(c_pool, c_chunk, c_rows, H, 0)
+        for n in range(1, AHEAD):
+            load_chunk(n)
 
         ident = const.tile([P, P], F32, name="ident")
         make_identity(nc, ident[:])
-        identb = const.tile([P, P], BF16, name="identb")
-        make_identity(nc, identb[:])
-        mhalf = const.tile([P, 2], F32, name="mhalf")
-        nc.gpsimd.memset(mhalf[:], -0.5)
-        epst = const.tile([P, 1], F32, name="epst")
-        nc.gpsimd.memset(epst[:], EPS)
+        plus_i = const.tile([P, P], BF16, name="plus_i")
+        make_identity(nc, plus_i[:])
+        minus_half = const.tile([P, 2], F32, name="minus_half")
+        nc.gpsimd.memset(minus_half[:], -0.5)
+        eps = const.tile([P, 1], F32, name="eps")
+        nc.gpsimd.memset(eps[:], EPS)
         ones = const.tile([P, P], BF16, name="ones")
         nc.vector.memset(ones[:], 1.0)
-        nidentb = const.tile([P, P], BF16, name="nidentb")
-        nc.vector.tensor_scalar(out=nidentb[:], in0=identb[:], scalar1=-1.0, scalar2=None, op0=ALU.mult)
+        minus_i = const.tile([P, P], BF16, name="minus_i")
+        nc.vector.tensor_scalar(out=minus_i[:], in0=plus_i[:], scalar1=-1.0, scalar2=None, op0=ALU.mult)
 
-        gw = const.tile([P, 3, 4 * H], BF16, name="gw", align_bytes=64)
-        wc = const.tile([P, 3, H], U32, name="wc", align_bytes=64)
-        ws = const.tile([P, 3, H], U8, name="ws", align_bytes=64)
-        gw_w = gw[:].bitcast(F32)
+        w_grouped = const.tile([P, 3, 4 * H], BF16, name="w_grouped", align_bytes=64)
+        w_words = const.tile([P, 3, H], U32, name="w_words", align_bytes=64)
+        w_scales = const.tile([P, 3, H], U8, name="w_scales", align_bytes=64)
 
-        def quant_w(s):
-            nc.vector.quantize_mx(out=wc[:, s, :].bitcast(FP8X4), scales=ws[:, s, :], in_=gw[:, s, :])
-
-        def prep_w(s, j, bank, on_scalar):
-            raw_w = (w_raw if s == 0 else u_raw)[:].bitcast(F32)
-            g = max(s - 1, 0)
+        def transpose_weight(n_pass, half, bank, on_scalar):
+            raw = (w_raw if n_pass == 0 else u_raw)[:].bitcast(F32)
+            first_word = 2 * P * max(n_pass - 1, 0)
             for u in range(2):
-                for fl in range(2):
+                for b in range(2):
                     nc.tensor.transpose(
-                        bank[:, u * 256 + fl * P:u * 256 + (fl + 1) * P],
-                        raw_w[:, 2 * j + fl, (2 * g + u) * P:(2 * g + u + 1) * P],
+                        bank[:, (2 * u + b) * P:(2 * u + b + 1) * P],
+                        raw[:, 2 * half + b, first_word + u * P:first_word + (u + 1) * P],
                         ident[:],
                     )
-            dst = gw_w[:, s, j * 512:(j + 1) * 512].rearrange("p (f u) -> p f u", u=2)
-            src = bank[:].rearrange("p (u f) -> p f u", u=2)
-            if on_scalar:
-                nc.scalar.copy(out=dst, in_=src)
-            else:
-                nc.vector.tensor_copy(out=dst, in_=src)
+            grouped = w_grouped[:].bitcast(F32)[:, n_pass, half * BANK:(half + 1) * BANK]
+            copy = nc.scalar.copy if on_scalar else nc.vector.tensor_copy
+            copy(out=grouped.rearrange("p (f u) -> p f u", u=2), in_=bank[:].rearrange("p (u f) -> p f u", u=2))
 
-        xt_t, ht_t, gx_t, gh_t, cx_t, sx_t, chh_t, shh_t = {}, {}, {}, {}, {}, {}, {}, {}
-        s4_t, p0_t, p1_t, nm_t, ss_t, r_t, a_t, b_t, d_t, o_t = {}, {}, {}, {}, {}, {}, {}, {}, {}, {}
+        def quantise_weight(n_pass):
+            nc.vector.quantize_mx(out=w_words[:, n_pass, :].bitcast(FP8X4), scales=w_scales[:, n_pass, :],
+                                  in_=w_grouped[:, n_pass, :])
 
-        def on_pe(i):
-            return i % 2 == 0
+        x_t, h_t, x_grouped, h_grouped, x_words, x_scales, h_words, h_scales = {}, {}, {}, {}, {}, {}, {}, {}
+        block_sums, prod0, prod1, neg_mean, sq_sum, rstd, ln0, ln1, diff, blend = {}, {}, {}, {}, {}, {}, {}, {}, {}, {}
 
-        def trx(i):
-            if not 0 <= i < NT:
+        def transpose_x(t):
+            if not 0 <= t < TILES:
                 return
-            xw = x_ch[i // CH][:].bitcast(F32)
-            xt = ps1.tile([P, 512], F32, name="xt", tag="xt")
-            for wb in range(4):
-                nc.tensor.transpose(xt[:, wb * P:(wb + 1) * P], xw[:, i % CH, wb * P:(wb + 1) * P], ident[:])
-            xt_t[i] = xt
+            words = x_chunk[t // CHUNK][:].bitcast(F32)
+            x_t[t] = psum_one.tile([P, BANK], F32, name="x_t", tag="x_t")
+            for b in range(4):
+                nc.tensor.transpose(x_t[t][:, b * P:(b + 1) * P], words[:, t % CHUNK, b * P:(b + 1) * P], ident[:])
 
-        def trh(J):
-            if not 0 <= J < ND:
+        def transpose_h(pair):
+            if not 0 <= pair < PAIRS:
                 return
-            ht = ps1.tile([P, 512], F32, name="ht", tag="ht")
-            for tau in range(2):
-                i = 2 * J + tau
-                hw = h_ch[i // CH][:].bitcast(F32)
+            h_t[pair] = psum_one.tile([P, BANK], F32, name="h_t", tag="h_t")
+            for s in range(2):
+                t = 2 * pair + s
+                words = h_chunk[t // CHUNK][:].bitcast(F32)
                 for u in range(2):
-                    nc.tensor.transpose(ht[:, (2 * tau + u) * P:(2 * tau + u + 1) * P], hw[:, i % CH, u * P:(u + 1) * P], ident[:])
-            ht_t[J] = ht
+                    nc.tensor.transpose(h_t[pair][:, (2 * s + u) * P:(2 * s + u + 1) * P],
+                                        words[:, t % CHUNK, u * P:(u + 1) * P], ident[:])
 
-        def evx(i):
-            if not 0 <= i < NT:
+        def regroup_x(t):
+            if not 0 <= t < TILES:
                 return
-            gx = grp.tile([P, IN], BF16, name="gx", tag="gx", align_bytes=64)
-            nc.scalar.copy(out=gx[:].bitcast(F32).rearrange("p (g r u) -> p g r u", g=2, u=2),
-                           in_=xt_t[i][:].rearrange("p (g u r) -> p g r u", g=2, u=2))
-            gx_t[i] = gx
+            x_grouped[t] = front.tile([P, IN], BF16, name="x_grouped", tag="x_grouped", align_bytes=64)
+            nc.scalar.copy(out=x_grouped[t][:].bitcast(F32).rearrange("p (g r u) -> p g r u", g=2, u=2),
+                           in_=x_t[t][:].rearrange("p (g u r) -> p g r u", g=2, u=2))
 
-        def evh(J):
-            if not 0 <= J < ND:
+        def regroup_h(pair):
+            if not 0 <= pair < PAIRS:
                 return
-            gh = grp.tile([P, 2 * H], BF16, name="gh", tag="gh", align_bytes=64, bufs=2)
-            nc.scalar.copy(out=gh[:].bitcast(F32).rearrange("p (t r u) -> p t r u", t=2, u=2),
-                           in_=ht_t[J][:].rearrange("p (t u r) -> p t r u", t=2, u=2))
-            gh_t[J] = gh
+            h_grouped[pair] = front.tile([P, 2 * H], BF16, name="h_grouped", tag="h_grouped", align_bytes=64)
+            nc.scalar.copy(out=h_grouped[pair][:].bitcast(F32).rearrange("p (s r u) -> p s r u", s=2, u=2),
+                           in_=h_t[pair][:].rearrange("p (s u r) -> p s r u", s=2, u=2))
 
-        def qh(J):
-            if not 0 <= J < ND:
+        def quantise_x(t):
+            if not 0 <= t < TILES:
                 return
-            chh = cod.tile([P, 256], U32, name="chh", tag="chh", align_bytes=64)
-            shh = cod.tile([P, 256], U8, name="shh", tag="shh", align_bytes=64)
-            nc.vector.quantize_mx(out=chh[:].bitcast(FP8X4), scales=shh[:], in_=gh_t[J][:])
-            chh_t[J], shh_t[J] = chh, shh
+            x_words[t] = front.tile([P, 2 * P], U32, name="x_words", tag="x_words", align_bytes=64)
+            x_scales[t] = front.tile([P, 2 * P], U8, name="x_scales", tag="x_scales", align_bytes=64)
+            nc.vector.quantize_mx(out=x_words[t][:].bitcast(FP8X4), scales=x_scales[t][:], in_=x_grouped[t][:])
 
-        def qx(i):
-            if not 0 <= i < NT:
+        def quantise_h(pair):
+            if not 0 <= pair < PAIRS:
                 return
-            cx = cod.tile([P, 256], U32, name="cx", tag="cx", align_bytes=64)
-            sx = cod.tile([P, 256], U8, name="sx", tag="sx", align_bytes=64)
-            nc.vector.quantize_mx(out=cx[:].bitcast(FP8X4), scales=sx[:], in_=gx_t[i][:])
-            cx_t[i], sx_t[i] = cx, sx
+            h_words[pair] = front.tile([P, 2 * P], U32, name="h_words", tag="h_words", align_bytes=64)
+            h_scales[pair] = front.tile([P, 2 * P], U8, name="h_scales", tag="h_scales", align_bytes=64)
+            nc.vector.quantize_mx(out=h_words[pair][:].bitcast(FP8X4), scales=h_scales[pair][:], in_=h_grouped[pair][:])
 
-        def mx(dst, lw, ls, s, cols, start, stop):
-            nc.tensor.matmul_mx(out=dst, lhsT=lw.bitcast(FP8X4), lhsT_scale=ls,
-                                rhs=wc[:, s, cols].bitcast(FP8X4), rhs_scale=ws[:, s, cols], start=start, stop=stop)
+        def mx_pass(acc, words, scales, n_pass, features, start, stop):
+            nc.tensor.matmul_mx(out=acc, lhsT=words.bitcast(FP8X4), lhsT_scale=scales,
+                                rhs=w_words[:, n_pass, features].bitcast(FP8X4), rhs_scale=w_scales[:, n_pass, features],
+                                start=start, stop=stop)
 
-        def mm(i):
-            if not 0 <= i < NT:
+        def products(t):
+            if not 0 <= t < TILES:
                 return
-            J, tau = i // 2, i % 2
-            hs = slice(tau * P, (tau + 1) * P)
-            hw_, hsc = chh_t[J][:, hs], shh_t[J][:, hs]
-            xw_ = [cx_t[i][:, g * P:(g + 1) * P] for g in range(2)]
-            xsc = [sx_t[i][:, g * P:(g + 1) * P] for g in range(2)]
-            s4 = ps1.tile([P, 2 * P], F32, name="s4", tag="s4")
-            for fb in range(4):
-                mx(s4[:, 0:P], hw_, hsc, 0, slice(fb * P, (fb + 1) * P), fb == 0, fb == 3)
+            rows_h = slice((t % 2) * P, (t % 2 + 1) * P)
+            operands = [(h_words[t // 2][:, rows_h], h_scales[t // 2][:, rows_h], 0)]
             for g in range(2):
-                for fb in range(4):
-                    mx(s4[:, P:2 * P], xw_[g], xsc[g], 1 + g, slice(fb * P, (fb + 1) * P), g == 0 and fb == 0, g == 1 and fb == 3)
-            p0 = ps3.tile([P, H], F32, name="p0", tag="p")
-            mx(p0[:], hw_, hsc, 0, slice(0, H), True, True)
-            p1 = ps3.tile([P, H], F32, name="p1", tag="p")
-            for g in range(2):
-                mx(p1[:], xw_[g], xsc[g], 1 + g, slice(0, H), g == 0, g == 1)
-            s4_t[i], p0_t[i], p1_t[i] = s4, p0, p1
+                operands.append((x_words[t][:, g * P:(g + 1) * P], x_scales[t][:, g * P:(g + 1) * P], 1 + g))
+            block_sums[t] = psum_one.tile([P, 2 * P], F32, name="block_sums", tag="block_sums")
+            for n, (words, scales, n_pass) in enumerate(operands):
+                for b in range(4):
+                    mx_pass(block_sums[t][:, min(n, 1) * P:(min(n, 1) + 1) * P], words, scales, n_pass,
+                            slice(b * P, (b + 1) * P), start=(n < 2 and b == 0), stop=(n != 1 and b == 3))
+            prod0[t] = psum_ring.tile([P, H], F32, name="prod0", tag="prod")
+            prod1[t] = psum_ring.tile([P, H], F32, name="prod1", tag="prod")
+            for n, (words, scales, n_pass) in enumerate(operands):
+                mx_pass((prod0[t] if n == 0 else prod1[t])[:], words, scales, n_pass, slice(0, H),
+                        start=(n < 2), stop=(n != 1))
 
-        def mean(i):
-            if not 0 <= i < NT:
+        def means(t):
+            if not 0 <= t < TILES:
                 return
-            nm = sml.tile([P, 2], F32, name="nm", tag="nm")
-            mj = wrk.tile([P, 2 * P], F32, name="mj", tag="mj", bufs=2)
-            for l in range(2):
-                nc.scalar.activation(out=mj[:, l * P:(l + 1) * P], in_=s4_t[i][:, l * P:(l + 1) * P], func=ACT.Identity,
-                                     scale=-1.0 / H, accum_out=nm[:, l:l + 1])
-            nm_t[i] = nm
+            neg_mean[t] = stats.tile([P, 2], F32, name="neg_mean", tag="neg_mean")
+            unused = work.tile([P, 2 * P], F32, name="unused", tag="unused", bufs=2)
+            for n in range(2):
+                nc.scalar.activation(out=unused[:, n * P:(n + 1) * P], in_=block_sums[t][:, n * P:(n + 1) * P],
+                                     func=ACT.Identity, scale=-1.0 / H, accum_out=neg_mean[t][:, n:n + 1])
 
-        def sq(i):
-            if not 0 <= i < NT:
+        def square_sums(t):
+            if not 0 <= t < TILES:
                 return
-            ss = sml.tile([P, 2], F32, name="ss", tag="ss")
-            a = wrk.tile([P, H], F32, name="a", tag="a")
-            b = wrk.tile([P, H], F32, name="b", tag="b", bufs=6)
-            nc.scalar.activation(out=a[:], in_=p0_t[i][:], func=ACT.Square, bias=nm_t[i][:, 0:1], accum_out=ss[:, 0:1])
-            nc.scalar.activation(out=b[:], in_=p1_t[i][:], func=ACT.Square, bias=nm_t[i][:, 1:2], accum_out=ss[:, 1:2])
-            ss_t[i], a_t[i], b_t[i] = ss, a, b
+            sq_sum[t] = stats.tile([P, 2], F32, name="sq_sum", tag="sq_sum")
+            ln0[t] = work.tile([P, H], F32, name="ln0", tag="ln0")
+            ln1[t] = work.tile([P, H], F32, name="ln1", tag="ln1", bufs=6)
+            for n, (prod, squares) in enumerate(((prod0[t], ln0[t]), (prod1[t], ln1[t]))):
+                nc.scalar.activation(out=squares[:], in_=prod[:], func=ACT.Square, bias=neg_mean[t][:, n:n + 1],
+                                     accum_out=sq_sum[t][:, n:n + 1])
 
-        def rs(i):
-            if not 0 <= i < NT:
+        def inverse_std(t):
+            if not 0 <= t < TILES:
                 return
-            v = sml.tile([P, 2], F32, name="v", tag="v")
-            r = sml.tile([P, 2], F32, name="r", tag="r")
-            nc.scalar.activation(out=v[:], in_=ss_t[i][:], func=ACT.Identity, scale=1.0 / H, bias=epst[:, 0:1])
-            nc.gpsimd.tensor_tensor(out=r[:], in0=v[:], in1=mhalf[:], op=ALU.pow)
-            r_t[i] = r
+            var_eps = stats.tile([P, 2], F32, name="var_eps", tag="var_eps")
+            rstd[t] = stats.tile([P, 2], F32, name="rstd", tag="rstd")
+            nc.scalar.activation(out=var_eps[:], in_=sq_sum[t][:], func=ACT.Identity, scale=1.0 / H, bias=eps[:, 0:1])
+            nc.gpsimd.tensor_tensor(out=rstd[t][:], in0=var_eps[:], in1=minus_half[:], op=ALU.pow)
 
-        def d_g(i):
-            if not 0 <= i < NT or on_pe(i):
+        def times_gamma(t, n):
+            if not 0 <= t < TILES:
                 return
-            dt_ = wrk.tile([P, H], F32, name="d", tag="d", bufs=3)
-            nc.gpsimd.tensor_tensor(out=dt_[:], in0=c_of(i), in1=h_of(i), op=ALU.subtract)
-            d_t[i] = dt_
+            prod, dst = ((prod0[t], ln0[t]), (prod1[t], ln1[t]))[n]
+            nc.vector.scalar_tensor_tensor(out=dst[:], in0=prod[:], scalar=neg_mean[t][:, n:n + 1],
+                                           in1=gamma[:, n * H:(n + 1) * H], op0=ALU.add, op1=ALU.mult)
 
-        def d_p(i):
-            if not 0 <= i < NT or not on_pe(i):
+        def add_norm0(t):
+            if 0 <= t < TILES:
+                nc.vector.scalar_tensor_tensor(out=ln0[t][:], in0=ln0[t][:], scalar=rstd[t][:, 0:1], in1=beta_sum[:],
+                                               op0=ALU.mult, op1=ALU.add)
+
+        def add_norm1(t):
+            if 0 <= t < TILES:
+                nc.vector.scalar_tensor_tensor(out=ln1[t][:], in0=ln1[t][:], scalar=rstd[t][:, 1:2], in1=ln0[t][:],
+                                               op0=ALU.mult, op1=ALU.add)
+
+        def gate(t):
+            if 0 <= t < TILES:
+                nc.scalar.activation(out=ln1[t][:], in_=ln1[t][:], func=ACT.Sigmoid)
+
+        def diff_on_tensor(t):
+            if not 0 <= t < TILES or t % 2 != 0:
                 return
-            dp = ps1.tile([P, H], F32, name="dp", tag="dd")
-            nc.tensor.matmul(out=dp[:], lhsT=identb[:], rhs=c_of(i), start=True, stop=False)
-            nc.tensor.matmul(out=dp[:], lhsT=nidentb[:], rhs=h_of(i), start=False, stop=True)
-            d_t[i] = dp
+            diff[t] = psum_one.tile([P, H], F32, name="diff_psum", tag="diff_psum")
+            nc.tensor.matmul(out=diff[t][:], lhsT=plus_i[:], rhs=c_of(t), start=True, stop=False)
+            nc.tensor.matmul(out=diff[t][:], lhsT=minus_i[:], rhs=h_of(t), start=False, stop=True)
 
-        def op_a(i):
-            if 0 <= i < NT:
-                nc.vector.scalar_tensor_tensor(out=a_t[i][:], in0=p0_t[i][:], scalar=nm_t[i][:, 0:1], in1=gam[:, 0:H], op0=ALU.add, op1=ALU.mult)
-
-        def op_b(i):
-            if 0 <= i < NT:
-                nc.vector.scalar_tensor_tensor(out=b_t[i][:], in0=p1_t[i][:], scalar=nm_t[i][:, 1:2], in1=gam[:, H:2 * H], op0=ALU.add, op1=ALU.mult)
-
-        def op_y(i):
-            if 0 <= i < NT:
-                nc.vector.scalar_tensor_tensor(out=a_t[i][:], in0=a_t[i][:], scalar=r_t[i][:, 0:1], in1=bs[:], op0=ALU.mult, op1=ALU.add)
-
-        def op_z(i):
-            if 0 <= i < NT:
-                nc.vector.scalar_tensor_tensor(out=b_t[i][:], in0=b_t[i][:], scalar=r_t[i][:, 1:2], in1=a_t[i][:], op0=ALU.mult, op1=ALU.add)
-
-        def sg(i):
-            if not 0 <= i < NT:
+        def diff_on_gpsimd(t):
+            if not 0 <= t < TILES or t % 2 != 1:
                 return
-            nc.scalar.activation(out=b_t[i][:], in_=b_t[i][:], func=ACT.Sigmoid)
+            diff[t] = work.tile([P, H], F32, name="diff", tag="diff", bufs=3)
+            nc.gpsimd.tensor_tensor(out=diff[t][:], in0=c_of(t), in1=h_of(t), op=ALU.subtract)
 
-        def op_e(i):
-            if not 0 <= i < NT:
+        def gate_times_diff(t):
+            if not 0 <= t < TILES:
                 return
-            J, tau = i // 2, i % 2
-            if tau == 0:
-                o_t[J] = opl.tile([P, 2, H], F32, name="o", tag="o")
-            nc.vector.tensor_tensor(out=o_t[J][:, tau, :], in0=b_t[i][:], in1=d_t[i][:], op=ALU.mult)
+            blend[t] = work.tile([P, H], F32, name="blend", tag="blend", bufs=6)
+            nc.vector.tensor_tensor(out=blend[t][:], in0=ln1[t][:], in1=diff[t][:], op=ALU.mult)
 
-        def op_o(i):
-            if not 0 <= i < NT:
+        def add_h_and_store(t):
+            if not 0 <= t < TILES:
                 return
-            J, tau = i // 2, i % 2
-            o = o_t[J]
-            if (on_pe(i) and i != NT - 2) or i == NT - 3:
-                nc.gpsimd.tensor_tensor(out=o[:, tau, :], in0=o[:, tau, :], in1=h_of(i), op=ALU.add)
-            else:
-                nc.vector.tensor_tensor(out=o[:, tau, :], in0=o[:, tau, :], in1=h_of(i), op=ALU.add)
-            if J == ND - 1:
-                nc.sync.dma_start(out=ov[:, i, :], in_=o[:, tau, :])
+            engine = nc.gpsimd if t % 2 == 0 else nc.vector
+            engine.tensor_tensor(out=blend[t][:], in0=blend[t][:], in1=h_of(t), op=ALU.add)
+            nc.sync.dma_start(out=out_rows[:, t, :], in_=blend[t][:])
 
-        def store(J):
-            if not 0 <= J < ND - 1:
-                return
-            nc.sync.dma_start(out=ov[:, 2 * J:2 * J + 2, :], in_=o_t[J][:])
+        transpose_h(0)
+        transpose_x(0)
+        regroup_h(0)
+        regroup_x(0)
+        quantise_h(0)
+        quantise_x(0)
+        transpose_weight(1, 0, psum_ring.tile([P, BANK], F32, name="w_t0", tag="prod"), True)
+        transpose_weight(1, 1, psum_ring.tile([P, BANK], F32, name="w_t1", tag="prod"), False)
+        transpose_weight(2, 0, psum_ring.tile([P, BANK], F32, name="w_t2", tag="prod"), True)
+        transpose_weight(2, 1, psum_one.tile([P, BANK], F32, name="w_t3", tag="diff_psum"), False)
+        quantise_weight(1)
+        transpose_weight(0, 0, psum_one.tile([P, BANK], F32, name="w_t4", tag="block_sums"), True)
+        transpose_weight(0, 1, psum_one.tile([P, BANK], F32, name="w_t5", tag="beta_sum"), False)
+        quantise_weight(2)
+        transpose_x(1)
+        transpose_h(1)
+        gamma = const.tile([P, 2 * H], F32, name="gamma")
+        for n in range(2):
+            spread = psum_ring.tile([P, H], F32, name="spread", tag="prod")
+            nc.tensor.matmul(out=spread[:], lhsT=ones[:], rhs=vectors[:, n, :], start=True, stop=True)
+            nc.vector.tensor_copy(out=gamma[:, n * H:(n + 1) * H], in_=spread[:])
+            if n == 0:
+                quantise_weight(0)
+        beta_sum = psum_one.tile([P, H], F32, name="beta_sum", tag="beta_sum")
+        nc.tensor.matmul(out=beta_sum[:], lhsT=ones[:], rhs=vectors[:, 2, :], start=True, stop=True)
+        products(0)
+        regroup_x(1)
+        regroup_h(1)
+        transpose_x(2)
+        transpose_h(2)
+        quantise_x(1)
+        quantise_h(1)
+        diff_on_gpsimd(1)
 
-        trh(0)
-        trx(0)
-        evh(0)
-        evx(0)
-        qh(0)
-        qx(0)
-        prep_w(1, 0, ps3.tile([P, 512], F32, name="wb0", tag="p"), True)
-        prep_w(1, 1, ps3.tile([P, 512], F32, name="wb1", tag="p"), False)
-        prep_w(2, 0, ps3.tile([P, 512], F32, name="wb2", tag="p"), True)
-        prep_w(2, 1, ps1.tile([P, 512], F32, name="wb3", tag="dd"), False)
-        quant_w(1)
-        prep_w(0, 0, ps1.tile([P, 512], F32, name="wb4", tag="s4"), True)
-        prep_w(0, 1, ps1.tile([P, 512], F32, name="wb5", tag="ht"), False)
-        quant_w(2)
-        trx(1)
-        gam = const.tile([P, 2 * H], F32, name="gam")
-        for s in range(2):
-            gp = ps3.tile([P, H], F32, name="gp", tag="p")
-            nc.tensor.matmul(out=gp[:], lhsT=ones[:], rhs=zt[:, s, :], start=True, stop=True)
-            if s == 0:
-                nc.vector.tensor_copy(out=gam[:, s * H:(s + 1) * H], in_=gp[:])
-                quant_w(0)
-            else:
-                nc.vector.tensor_copy(out=gam[:, s * H:(s + 1) * H], in_=gp[:])
-        bs = ps1.tile([P, H], F32, name="bs", tag="bs")
-        nc.tensor.matmul(out=bs[:], lhsT=ones[:], rhs=zt[:, 2, :], start=True, stop=True)
-        mm(0)
-        evx(1)
-        trx(2)
-        trh(1)
-        qx(1)
-        d_g(1)
-
-        for i in range(NT + 5):
+        for i in range(TILES + 4):
             even = i % 2 == 0
-            if i % CH == 0 and i // CH + 3 < NCH:
-                load_h(i // CH + 3)
-                load_x(i // CH + 3)
-                load_c(i // CH + 3)
-            d_p(i - 4)
-            mean(i)
-            sq(i)
-            rs(i)
-            op_a(i)
-            op_y(i - 2)
-            op_b(i)
-            op_z(i - 2)
-            evx(i + 2)
+            if i % CHUNK == 0 and i // CHUNK + AHEAD < CHUNKS:
+                load_chunk(i // CHUNK + AHEAD)
+            diff_on_tensor(i - 4)
+            means(i)
+            square_sums(i)
+            inverse_std(i)
+            times_gamma(i, 0)
+            add_norm0(i - 2)
+            times_gamma(i, 1)
+            add_norm1(i - 2)
+            regroup_x(i + 2)
             if even:
-                evh(i // 2 + 1)
-            sg(i - 3)
-            op_e(i - 4)
-            qx(i + 2)
+                regroup_h(i // 2 + 2)
+            gate(i - 3)
+            gate_times_diff(i - 4)
+            quantise_x(i + 2)
             if even:
-                qh(i // 2 + 1)
-            op_o(i - 4)
-            d_g(i + 2)
+                quantise_h(i // 2 + 2)
+            add_h_and_store(i - 4)
+            diff_on_gpsimd(i + 2)
+            products(i + 1)
+            transpose_x(i + 3)
             if not even:
-                store((i - 5) // 2)
-            mm(i + 1)
-            trx(i + 3)
-            if not even:
-                trh((i + 3) // 2)
+                transpose_h((i + 5) // 2)

@@ -36,7 +36,6 @@ def tile_layernormgrucell_pb_t_kernel(tc, x, h, c, W_u, U_u, ln_gamma, ln_beta, 
         stats = ctx.enter_context(tc.tile_pool(name="stats", bufs=6))
         psum_ring = ctx.enter_context(tc.psum_pool(name="psum_ring", bufs=3))
         psum_one = ctx.enter_context(tc.psum_pool(name="psum_one", bufs=1))
-        ctx.enter_context(tc.manual_schedule())
 
         x_rows = x.rearrange("(p t) k -> p t k", t=TILES)
         h_rows = h.rearrange("(p t) k -> p t k", t=TILES)

@@ -292,7 +292,8 @@ def tile_layernormgrucell_pb_t_kernel(tc, x, h, c, W_u, U_u, ln_gamma, ln_beta, 
         quantise_h(1)
         diff_on_gpsimd(1)
 
-        for i in range(TILES + 4):
+        ctx.enter_context(tc.manual_schedule(engines={mybir.EngineType.DVE, mybir.EngineType.Pool}))
+        for i in range(TILES + 6):
             even = i % 2 == 0
             if i % CHUNK == 0 and i // CHUNK + AHEAD < CHUNKS:
                 load_chunk(i // CHUNK + AHEAD)
@@ -308,11 +309,14 @@ def tile_layernormgrucell_pb_t_kernel(tc, x, h, c, W_u, U_u, ln_gamma, ln_beta, 
             if even:
                 regroup_h(i // 2 + 2)
             gate(i - 3)
-            gate_times_diff(i - 4)
+            if not even:
+                add_h_and_store(i - 6)
             quantise_x(i + 2)
             if even:
                 quantise_h(i // 2 + 2)
-            add_h_and_store(i - 4)
+            gate_times_diff(i - 4)
+            if even:
+                add_h_and_store(i - 4)
             diff_on_gpsimd(i + 2)
             products(i + 1)
             transpose_x(i + 3)

@@ -62,14 +62,20 @@ def tile_layernormgrucell_pb_t_kernel(tc, x, h, c, W_u, U_u, ln_gamma, ln_beta, 
 
         vectors = const.tile([P, 3, H], BF16, name="vectors")
         nc.vector.memset(vectors[:].bitcast(I32), 0)
-        load(h_pool, h_chunk, h_rows, H, 0, 0, 2)
-        load(x_pool, x_chunk, x_rows, IN, 0, 0, 2)
+        load(h_pool, h_chunk, h_rows, H, 0, 0, 1)
+        load(x_pool, x_chunk, x_rows, IN, 0, 0, 1)
+        u_raw = const.tile([P, 4, IN], BF16, name="u_raw")
+        w_raw = const.tile([P, 4, H], BF16, name="w_raw")
+        for half in range(2):
+            nc.sync.dma_start(out=u_raw[:, 2 * half:2 * half + 2, :],
+                              in_=U_u.rearrange("(b p) k -> p b k", p=P)[:, 2 * half:2 * half + 2, :])
         nc.sync.dma_start(out=vectors[0:1, 0:2, :], in_=ln_gamma.rearrange("(o g) f -> o g f", o=1))
         nc.sync.dma_start(out=vectors[0:2, 2, :], in_=ln_beta)
-        u_raw = const.tile([P, 4, IN], BF16, name="u_raw")
-        nc.sync.dma_start(out=u_raw[:], in_=U_u.rearrange("(b p) k -> p b k", p=P))
-        w_raw = const.tile([P, 4, H], BF16, name="w_raw")
-        nc.sync.dma_start(out=w_raw[:], in_=W_u.rearrange("(b p) k -> p b k", p=P))
+        for half in range(2):
+            nc.sync.dma_start(out=w_raw[:, 2 * half:2 * half + 2, :],
+                              in_=W_u.rearrange("(b p) k -> p b k", p=P)[:, 2 * half:2 * half + 2, :])
+        load(h_pool, h_chunk, h_rows, H, 0, 1, 2)
+        load(x_pool, x_chunk, x_rows, IN, 0, 1, 2)
         load(h_pool, h_chunk, h_rows, H, 0, 2, CHUNK)
         load(x_pool, x_chunk, x_rows, IN, 0, 2, CHUNK)
         load(c_pool, c_chunk, c_rows, H, 0)
@@ -107,9 +113,10 @@ def tile_layernormgrucell_pb_t_kernel(tc, x, h, c, W_u, U_u, ln_gamma, ln_beta, 
             copy = nc.scalar.copy if on_scalar else nc.vector.tensor_copy
             copy(out=grouped.rearrange("p (f u) -> p f u", u=2), in_=bank[:].rearrange("p (u f) -> p f u", u=2))
 
-        def quantise_weight(n_pass):
-            nc.vector.quantize_mx(out=w_words[:, n_pass, :].bitcast(FP8X4), scales=w_scales[:, n_pass, :],
-                                  in_=w_grouped[:, n_pass, :])
+        def quantise_weight(n_pass, half):
+            features = slice(half * 2 * P, (half + 1) * 2 * P)
+            nc.vector.quantize_mx(out=w_words[:, n_pass, features].bitcast(FP8X4), scales=w_scales[:, n_pass, features],
+                                  in_=w_grouped[:, n_pass, half * 2 * H:(half + 1) * 2 * H])
 
         x_t, h_t, x_grouped, h_grouped, x_words, x_scales, h_words, h_scales = {}, {}, {}, {}, {}, {}, {}, {}
         block_sums, prod0, prod1, neg_mean, sq_sum, rstd, ln0, ln1, diff, blend = {}, {}, {}, {}, {}, {}, {}, {}, {}, {}
@@ -122,30 +129,32 @@ def tile_layernormgrucell_pb_t_kernel(tc, x, h, c, W_u, U_u, ln_gamma, ln_beta, 
             for b in range(4):
                 nc.tensor.transpose(x_t[t][:, b * P:(b + 1) * P], words[:, t % CHUNK, b * P:(b + 1) * P], ident[:])
 
-        def transpose_h(pair):
+        def transpose_h(pair, parts=(0, 1)):
             if not 0 <= pair < PAIRS:
                 return
             h_t[pair] = psum_one.tile([P, BANK], F32, name="h_t", tag="h_t")
-            for s in range(2):
+            for s in parts:
                 t = 2 * pair + s
                 words = h_chunk[t // CHUNK][:].bitcast(F32)
                 for u in range(2):
                     nc.tensor.transpose(h_t[pair][:, (2 * s + u) * P:(2 * s + u + 1) * P],
                                         words[:, t % CHUNK, u * P:(u + 1) * P], ident[:])
 
-        def regroup_x(t):
+        def regroup_x(t, copy=nc.scalar.copy):
             if not 0 <= t < TILES:
                 return
             x_grouped[t] = front.tile([P, IN], BF16, name="x_grouped", tag="x_grouped", align_bytes=64)
-            nc.scalar.copy(out=x_grouped[t][:].bitcast(F32).rearrange("p (g r u) -> p g r u", g=2, u=2),
-                           in_=x_t[t][:].rearrange("p (g u r) -> p g r u", g=2, u=2))
+            copy(out=x_grouped[t][:].bitcast(F32).rearrange("p (g r u) -> p g r u", g=2, u=2),
+                 in_=x_t[t][:].rearrange("p (g u r) -> p g r u", g=2, u=2))
 
-        def regroup_h(pair):
+        def regroup_h(pair, parts=(0, 1), copy=nc.scalar.copy):
             if not 0 <= pair < PAIRS:
                 return
-            h_grouped[pair] = front.tile([P, 2 * H], BF16, name="h_grouped", tag="h_grouped", align_bytes=64)
-            nc.scalar.copy(out=h_grouped[pair][:].bitcast(F32).rearrange("p (s r u) -> p s r u", s=2, u=2),
-                           in_=h_t[pair][:].rearrange("p (s u r) -> p s r u", s=2, u=2))
+            if parts[0] == 0:
+                h_grouped[pair] = front.tile([P, 2 * H], BF16, name="h_grouped", tag="h_grouped", align_bytes=64)
+            words = slice(parts[0] * 2 * P, (parts[-1] + 1) * 2 * P)
+            copy(out=h_grouped[pair][:].bitcast(F32)[:, words].rearrange("p (s r u) -> p s r u", u=2, r=P),
+                 in_=h_t[pair][:, words].rearrange("p (s u r) -> p s r u", u=2, r=P))
 
         def quantise_x(t):
             if not 0 <= t < TILES:
@@ -154,12 +163,15 @@ def tile_layernormgrucell_pb_t_kernel(tc, x, h, c, W_u, U_u, ln_gamma, ln_beta, 
             x_scales[t] = front.tile([P, 2 * P], U8, name="x_scales", tag="x_scales", align_bytes=64)
             nc.vector.quantize_mx(out=x_words[t][:].bitcast(FP8X4), scales=x_scales[t][:], in_=x_grouped[t][:])
 
-        def quantise_h(pair):
+        def quantise_h(pair, parts=(0, 1)):
             if not 0 <= pair < PAIRS:
                 return
-            h_words[pair] = front.tile([P, 2 * P], U32, name="h_words", tag="h_words", align_bytes=64)
-            h_scales[pair] = front.tile([P, 2 * P], U8, name="h_scales", tag="h_scales", align_bytes=64)
-            nc.vector.quantize_mx(out=h_words[pair][:].bitcast(FP8X4), scales=h_scales[pair][:], in_=h_grouped[pair][:])
+            if parts[0] == 0:
+                h_words[pair] = front.tile([P, 2 * P], U32, name="h_words", tag="h_words", align_bytes=64)
+                h_scales[pair] = front.tile([P, 2 * P], U8, name="h_scales", tag="h_scales", align_bytes=64)
+            rows = slice(parts[0] * P, (parts[-1] + 1) * P)
+            nc.vector.quantize_mx(out=h_words[pair][:, rows].bitcast(FP8X4), scales=h_scales[pair][:, rows],
+                                  in_=h_grouped[pair][:, parts[0] * H:(parts[-1] + 1) * H])
 
         def mx_pass(acc, words, scales, n_pass, features, start, stop):
             nc.tensor.matmul_mx(out=acc, lhsT=words.bitcast(FP8X4), lhsT_scale=scales,
@@ -174,7 +186,7 @@ def tile_layernormgrucell_pb_t_kernel(tc, x, h, c, W_u, U_u, ln_gamma, ln_beta, 
             for g in range(2):
                 operands.append((x_words[t][:, g * P:(g + 1) * P], x_scales[t][:, g * P:(g + 1) * P], 1 + g))
             block_sums[t] = psum_one.tile([P, 2 * P], F32, name="block_sums", tag="block_sums")
-            for n, (words, scales, n_pass) in enumerate(operands):
+            for n, (words, scales, n_pass) in list(enumerate(operands))[1:] + list(enumerate(operands))[:1]:
                 for b in range(4):
                     mx_pass(block_sums[t][:, min(n, 1) * P:(min(n, 1) + 1) * P], words, scales, n_pass,
                             slice(b * P, (b + 1) * P), start=(n < 2 and b == 0), stop=(n != 1 and b == 3))
@@ -258,38 +270,43 @@ def tile_layernormgrucell_pb_t_kernel(tc, x, h, c, W_u, U_u, ln_gamma, ln_beta, 
             engine.tensor_tensor(out=blend[t][:], in0=blend[t][:], in1=h_of(t), op=ALU.add)
             nc.sync.dma_start(out=out_rows[:, t, :], in_=blend[t][:])
 
-        transpose_h(0)
+        ctx.enter_context(tc.manual_schedule(engines={mybir.EngineType.DVE, mybir.EngineType.Pool}))
+        transpose_h(0, (0,))
         transpose_x(0)
-        regroup_h(0)
+        regroup_h(0, (0,))
         regroup_x(0)
-        quantise_h(0)
+        quantise_h(0, (0,))
         quantise_x(0)
         transpose_weight(1, 0, psum_ring.tile([P, BANK], F32, name="w_t0", tag="prod"), True)
-        transpose_weight(1, 1, psum_ring.tile([P, BANK], F32, name="w_t1", tag="prod"), False)
-        transpose_weight(2, 0, psum_ring.tile([P, BANK], F32, name="w_t2", tag="prod"), True)
+        transpose_weight(2, 0, psum_ring.tile([P, BANK], F32, name="w_t1", tag="prod"), False)
+        quantise_weight(1, 0)
+        transpose_weight(1, 1, psum_ring.tile([P, BANK], F32, name="w_t2", tag="prod"), True)
+        quantise_weight(2, 0)
         transpose_weight(2, 1, psum_one.tile([P, BANK], F32, name="w_t3", tag="diff_psum"), False)
-        quantise_weight(1)
-        transpose_weight(0, 0, psum_one.tile([P, BANK], F32, name="w_t4", tag="block_sums"), True)
-        transpose_weight(0, 1, psum_one.tile([P, BANK], F32, name="w_t5", tag="beta_sum"), False)
-        quantise_weight(2)
-        transpose_x(1)
-        transpose_h(1)
+        quantise_weight(1, 1)
+        transpose_weight(0, 0, psum_one.tile([P, BANK], F32, name="w_t4", tag="beta_sum"), True)
+        quantise_weight(2, 1)
+        transpose_weight(0, 1, psum_ring.tile([P, BANK], F32, name="w_t5", tag="prod"), True)
+        quantise_weight(0, 0)
         gamma = const.tile([P, 2 * H], F32, name="gamma")
+        spread = {}
         for n in range(2):
-            spread = psum_ring.tile([P, H], F32, name="spread", tag="prod")
-            nc.tensor.matmul(out=spread[:], lhsT=ones[:], rhs=vectors[:, n, :], start=True, stop=True)
-            nc.vector.tensor_copy(out=gamma[:, n * H:(n + 1) * H], in_=spread[:])
-            if n == 0:
-                quantise_weight(0)
+            spread[n] = psum_ring.tile([P, H], F32, name="spread", tag="prod")
+            nc.tensor.matmul(out=spread[n][:], lhsT=ones[:], rhs=vectors[:, n, :], start=True, stop=True)
+        quantise_weight(0, 1)
+        nc.scalar.copy(out=gamma[:, 0:H], in_=spread[0][:])
+        transpose_x(1)
+        transpose_h(0, (1,))
+        products(0)
+        nc.vector.tensor_copy(out=gamma[:, H:2 * H], in_=spread[1][:])
+        regroup_x(1, nc.vector.tensor_copy)
+        regroup_h(0, (1,), nc.vector.tensor_copy)
+        transpose_x(2)
+        transpose_h(1)
         beta_sum = psum_one.tile([P, H], F32, name="beta_sum", tag="beta_sum")
         nc.tensor.matmul(out=beta_sum[:], lhsT=ones[:], rhs=vectors[:, 2, :], start=True, stop=True)
-        products(0)
-        regroup_x(1)
-        regroup_h(1)
-        transpose_x(2)
-        transpose_h(2)
         quantise_x(1)
-        quantise_h(1)
+        quantise_h(0, (1,))
         diff_on_gpsimd(1)
 
         ctx.enter_context(tc.manual_schedule(engines={mybir.EngineType.DVE, mybir.EngineType.Pool}))
@@ -297,6 +314,7 @@ def tile_layernormgrucell_pb_t_kernel(tc, x, h, c, W_u, U_u, ln_gamma, ln_beta, 
             even = i % 2 == 0
             if i % CHUNK == 0 and i // CHUNK + AHEAD < CHUNKS:
                 load_chunk(i // CHUNK + AHEAD)
+            copy = nc.vector.tensor_copy if i < 2 else nc.scalar.copy
             diff_on_tensor(i - 4)
             means(i)
             square_sums(i)
@@ -305,15 +323,15 @@ def tile_layernormgrucell_pb_t_kernel(tc, x, h, c, W_u, U_u, ln_gamma, ln_beta, 
             add_norm0(i - 2)
             times_gamma(i, 1)
             add_norm1(i - 2)
-            regroup_x(i + 2)
+            regroup_x(i + 2, copy)
             if even:
-                regroup_h(i // 2 + 2)
+                regroup_h(i // 2 + 1, copy=copy)
             gate(i - 3)
             if not even:
                 add_h_and_store(i - 6)
             quantise_x(i + 2)
             if even:
-                quantise_h(i // 2 + 2)
+                quantise_h(i // 2 + 1)
             gate_times_diff(i - 4)
             if even:
                 add_h_and_store(i - 4)
@@ -321,4 +339,4 @@ def tile_layernormgrucell_pb_t_kernel(tc, x, h, c, W_u, U_u, ln_gamma, ln_beta, 
             products(i + 1)
             transpose_x(i + 3)
             if not even:
-                transpose_h((i + 5) // 2)
+                transpose_h((i + 3) // 2)

@@ -31,7 +31,7 @@ def tile_layernormgrucell_pb_t_kernel(tc, x, h, c, W_u, U_u, ln_gamma, ln_beta, 
         x_pool = ctx.enter_context(tc.tile_pool(name="x_pool", bufs=AHEAD + 1))
         h_pool = ctx.enter_context(tc.tile_pool(name="h_pool", bufs=CHUNKS))
         c_pool = ctx.enter_context(tc.tile_pool(name="c_pool", bufs=AHEAD + 2))
-        front = ctx.enter_context(tc.tile_pool(name="front", bufs=3))
+        front = ctx.enter_context(tc.tile_pool(name="front", bufs=4))
         work = ctx.enter_context(tc.tile_pool(name="work", bufs=4))
         stats = ctx.enter_context(tc.tile_pool(name="stats", bufs=6))
         psum_ring = ctx.enter_context(tc.psum_pool(name="psum_ring", bufs=3))
@@ -51,8 +51,11 @@ def tile_layernormgrucell_pb_t_kernel(tc, x, h, c, W_u, U_u, ln_gamma, ln_beta, 
 
         def load_chunk(n):
             load(h_pool, h_chunk, h_rows, H, n)
-            load(x_pool, x_chunk, x_rows, IN, n)
+            if n == 1:
+                load(x_pool, x_chunk, x_rows, IN, n)
             load(c_pool, c_chunk, c_rows, H, n)
+            if n != 1:
+                load(x_pool, x_chunk, x_rows, IN, n)
 
         def h_of(t):
             return h_chunk[t // CHUNK][:, t % CHUNK, :]
@@ -86,7 +89,7 @@ def tile_layernormgrucell_pb_t_kernel(tc, x, h, c, W_u, U_u, ln_gamma, ln_beta, 
         make_identity(nc, ident[:])
         plus_i = const.tile([P, P], BF16, name="plus_i")
         make_identity(nc, plus_i[:])
-        minus_half = const.tile([P, 2], F32, name="minus_half")
+        minus_half = const.tile([P, 4], F32, name="minus_half")
         nc.gpsimd.memset(minus_half[:], -0.5)
         eps = const.tile([P, 1], F32, name="eps")
         nc.gpsimd.memset(eps[:], EPS)
@@ -178,23 +181,30 @@ def tile_layernormgrucell_pb_t_kernel(tc, x, h, c, W_u, U_u, ln_gamma, ln_beta, 
                                 rhs=w_words[:, n_pass, features].bitcast(FP8X4), rhs_scale=w_scales[:, n_pass, features],
                                 start=start, stop=stop)
 
-        def products(t):
-            if not 0 <= t < TILES:
-                return
+        def operands_of(t):
             rows_h = slice((t % 2) * P, (t % 2 + 1) * P)
             operands = [(h_words[t // 2][:, rows_h], h_scales[t // 2][:, rows_h], 0)]
             for g in range(2):
                 operands.append((x_words[t][:, g * P:(g + 1) * P], x_scales[t][:, g * P:(g + 1) * P], 1 + g))
+            return operands
+
+        def sums_of_blocks(t):
+            if not 0 <= t < TILES:
+                return
             block_sums[t] = psum_one.tile([P, 2 * P], F32, name="block_sums", tag="block_sums")
-            for n, (words, scales, n_pass) in list(enumerate(operands))[1:] + list(enumerate(operands))[:1]:
+            for n, (words, scales, n_pass) in list(enumerate(operands_of(t)))[1:] + list(enumerate(operands_of(t)))[:1]:
                 for b in range(4):
                     mx_pass(block_sums[t][:, min(n, 1) * P:(min(n, 1) + 1) * P], words, scales, n_pass,
                             slice(b * P, (b + 1) * P), start=(n < 2 and b == 0), stop=(n != 1 and b == 3))
-            prod0[t] = psum_ring.tile([P, H], F32, name="prod0", tag="prod")
-            prod1[t] = psum_ring.tile([P, H], F32, name="prod1", tag="prod")
-            for n, (words, scales, n_pass) in enumerate(operands):
-                mx_pass((prod0[t] if n == 0 else prod1[t])[:], words, scales, n_pass, slice(0, H),
-                        start=(n < 2), stop=(n != 1))
+
+        def product(t, n):
+            if not 0 <= t < TILES:
+                return
+            prod = psum_ring.tile([P, H], F32, name="prod", tag="prod")
+            (prod0, prod1)[n][t] = prod
+            passes = operands_of(t)[:1] if n == 0 else operands_of(t)[1:]
+            for j, (words, scales, n_pass) in enumerate(passes):
+                mx_pass(prod[:], words, scales, n_pass, slice(0, H), start=(j == 0), stop=(j == len(passes) - 1))
 
         def means(t):
             if not 0 <= t < TILES:
@@ -205,23 +215,31 @@ def tile_layernormgrucell_pb_t_kernel(tc, x, h, c, W_u, U_u, ln_gamma, ln_beta, 
                 nc.scalar.activation(out=unused[:, n * P:(n + 1) * P], in_=block_sums[t][:, n * P:(n + 1) * P],
                                      func=ACT.Identity, scale=-1.0 / H, accum_out=neg_mean[t][:, n:n + 1])
 
-        def square_sums(t):
+        def square_sum(t, n):
             if not 0 <= t < TILES:
                 return
-            sq_sum[t] = stats.tile([P, 2], F32, name="sq_sum", tag="sq_sum")
-            ln0[t] = work.tile([P, H], F32, name="ln0", tag="ln0")
-            ln1[t] = work.tile([P, H], F32, name="ln1", tag="ln1", bufs=6)
-            for n, (prod, squares) in enumerate(((prod0[t], ln0[t]), (prod1[t], ln1[t]))):
-                nc.scalar.activation(out=squares[:], in_=prod[:], func=ACT.Square, bias=neg_mean[t][:, n:n + 1],
-                                     accum_out=sq_sum[t][:, n:n + 1])
+            pair = t // 2
+            if t % 2 == 0 and n == 0:
+                sq_sum[pair] = stats.tile([P, 4], F32, name="sq_sum", tag="sq_sum")
+            if n == 0:
+                ln0[t] = work.tile([P, H], F32, name="ln0", tag="ln0", bufs=6)
+            else:
+                ln1[t] = work.tile([P, H], F32, name="ln1", tag="ln1", bufs=8)
+            prod, squares = (prod0[t], ln0[t]) if n == 0 else (prod1[t], ln1[t])
+            column = 2 * (t % 2) + n
+            nc.scalar.activation(out=squares[:], in_=prod[:], func=ACT.Square, bias=neg_mean[t][:, n:n + 1],
+                                 accum_out=sq_sum[pair][:, column:column + 1])
 
-        def inverse_std(t):
-            if not 0 <= t < TILES:
+        def inverse_stds(pair):
+            if not 0 <= pair < PAIRS:
                 return
-            var_eps = stats.tile([P, 2], F32, name="var_eps", tag="var_eps")
-            rstd[t] = stats.tile([P, 2], F32, name="rstd", tag="rstd")
-            nc.scalar.activation(out=var_eps[:], in_=sq_sum[t][:], func=ACT.Identity, scale=1.0 / H, bias=eps[:, 0:1])
-            nc.gpsimd.tensor_tensor(out=rstd[t][:], in0=var_eps[:], in1=minus_half[:], op=ALU.pow)
+            var_eps = stats.tile([P, 4], F32, name="var_eps", tag="var_eps")
+            rstd[pair] = stats.tile([P, 4], F32, name="rstd", tag="rstd")
+            nc.scalar.activation(out=var_eps[:], in_=sq_sum[pair][:], func=ACT.Identity, scale=1.0 / H, bias=eps[:, 0:1])
+            nc.gpsimd.tensor_tensor(out=rstd[pair][:], in0=var_eps[:], in1=minus_half[:], op=ALU.pow)
+
+        def rstd_of(t, n):
+            return rstd[t // 2][:, 2 * (t % 2) + n:2 * (t % 2) + n + 1]
 
         def times_gamma(t, n):
             if not 0 <= t < TILES:
@@ -232,12 +250,12 @@ def tile_layernormgrucell_pb_t_kernel(tc, x, h, c, W_u, U_u, ln_gamma, ln_beta, 
 
         def add_norm0(t):
             if 0 <= t < TILES:
-                nc.vector.scalar_tensor_tensor(out=ln0[t][:], in0=ln0[t][:], scalar=rstd[t][:, 0:1], in1=beta_sum[:],
+                nc.vector.scalar_tensor_tensor(out=ln0[t][:], in0=ln0[t][:], scalar=rstd_of(t, 0), in1=beta_sum[:],
                                                op0=ALU.mult, op1=ALU.add)
 
         def add_norm1(t):
             if 0 <= t < TILES:
-                nc.vector.scalar_tensor_tensor(out=ln1[t][:], in0=ln1[t][:], scalar=rstd[t][:, 1:2], in1=ln0[t][:],
+                nc.vector.scalar_tensor_tensor(out=ln1[t][:], in0=ln1[t][:], scalar=rstd_of(t, 1), in1=ln0[t][:],
                                                op0=ALU.mult, op1=ALU.add)
 
         def gate(t):
@@ -251,24 +269,28 @@ def tile_layernormgrucell_pb_t_kernel(tc, x, h, c, W_u, U_u, ln_gamma, ln_beta, 
             nc.tensor.matmul(out=diff[t][:], lhsT=plus_i[:], rhs=c_of(t), start=True, stop=False)
             nc.tensor.matmul(out=diff[t][:], lhsT=minus_i[:], rhs=h_of(t), start=False, stop=True)
 
-        def diff_on_gpsimd(t):
+        def odd_diff(t, engine, first=0, last=H):
             if not 0 <= t < TILES or t % 2 != 1:
                 return
-            diff[t] = work.tile([P, H], F32, name="diff", tag="diff", bufs=3)
-            nc.gpsimd.tensor_tensor(out=diff[t][:], in0=c_of(t), in1=h_of(t), op=ALU.subtract)
+            if t not in diff:
+                diff[t] = work.tile([P, H], F32, name="diff", tag="diff", bufs=6)
+            engine.tensor_tensor(out=diff[t][:, first:last], in0=c_of(t)[:, first:last], in1=h_of(t)[:, first:last],
+                                 op=ALU.subtract)
 
         def gate_times_diff(t):
             if not 0 <= t < TILES:
                 return
-            blend[t] = work.tile([P, H], F32, name="blend", tag="blend", bufs=6)
-            nc.vector.tensor_tensor(out=blend[t][:], in0=ln1[t][:], in1=diff[t][:], op=ALU.mult)
+            if t % 2 == 0:
+                blend[t // 2] = work.tile([P, 2, H], F32, name="blend", tag="blend", bufs=4)
+            nc.vector.tensor_tensor(out=blend[t // 2][:, t % 2, :], in0=ln1[t][:], in1=diff[t][:], op=ALU.mult)
 
-        def add_h_and_store(t):
-            if not 0 <= t < TILES:
+        def add_h_and_store(engine, first, n):
+            if not 0 <= first < TILES:
                 return
-            engine = nc.gpsimd if t % 2 == 0 else nc.vector
-            engine.tensor_tensor(out=blend[t][:], in0=blend[t][:], in1=h_of(t), op=ALU.add)
-            nc.sync.dma_start(out=out_rows[:, t, :], in_=blend[t][:])
+            y = blend[first // 2][:, first % 2:first % 2 + n, :]
+            h_rows_of = h_chunk[first // CHUNK][:, first % CHUNK:first % CHUNK + n, :]
+            engine.tensor_tensor(out=y, in0=y, in1=h_rows_of, op=ALU.add)
+            nc.sync.dma_start(out=out_rows[:, first:first + n, :], in_=y)
 
         ctx.enter_context(tc.manual_schedule(engines={mybir.EngineType.DVE, mybir.EngineType.Pool}))
         transpose_h(0, (0,))
@@ -295,48 +317,125 @@ def tile_layernormgrucell_pb_t_kernel(tc, x, h, c, W_u, U_u, ln_gamma, ln_beta, 
             nc.tensor.matmul(out=spread[n][:], lhsT=ones[:], rhs=vectors[:, n, :], start=True, stop=True)
         quantise_weight(0, 1)
         nc.scalar.copy(out=gamma[:, 0:H], in_=spread[0][:])
-        transpose_x(1)
-        transpose_h(0, (1,))
-        products(0)
-        nc.vector.tensor_copy(out=gamma[:, H:2 * H], in_=spread[1][:])
-        regroup_x(1, nc.vector.tensor_copy)
-        regroup_h(0, (1,), nc.vector.tensor_copy)
-        transpose_x(2)
-        transpose_h(1)
         beta_sum = psum_one.tile([P, H], F32, name="beta_sum", tag="beta_sum")
         nc.tensor.matmul(out=beta_sum[:], lhsT=ones[:], rhs=vectors[:, 2, :], start=True, stop=True)
+        nc.vector.tensor_copy(out=gamma[:, H:2 * H], in_=spread[1][:])
+        transpose_x(1)
+        transpose_h(0, (1,))
+        sums_of_blocks(0)
+        product(0, 0)
+        product(0, 1)
+        regroup_x(1, nc.vector.tensor_copy)
+        regroup_h(0, (1,), nc.vector.tensor_copy)
+        means(0)
+        square_sum(0, 0)
+        square_sum(0, 1)
         quantise_x(1)
         quantise_h(0, (1,))
-        diff_on_gpsimd(1)
+        transpose_x(2)
+        transpose_h(1)
+        sums_of_blocks(1)
+        product(1, 0)
+        means(1)
+        square_sum(1, 0)
+        odd_diff(1, nc.vector)
+        times_gamma(0, 0)
+        times_gamma(0, 1)
+        product(1, 1)
+        square_sum(1, 1)
+        inverse_stds(0)
+        regroup_x(2, nc.vector.tensor_copy)
+        regroup_h(1, copy=nc.vector.tensor_copy)
+        quantise_x(2)
+        quantise_h(1)
+        transpose_x(3)
+        sums_of_blocks(2)
+        times_gamma(1, 0)
+        times_gamma(1, 1)
+        product(2, 0)
+        product(2, 1)
+        means(2)
+        square_sum(2, 0)
+        square_sum(2, 1)
+        regroup_x(3, nc.vector.tensor_copy)
+        odd_diff(3, nc.vector)
+        transpose_x(4)
+        transpose_h(2)
+        quantise_x(3)
+        sums_of_blocks(3)
+        regroup_x(4, nc.vector.tensor_copy)
+        regroup_h(2)
+        product(3, 0)
+        means(3)
+        square_sum(3, 0)
+        transpose_x(5)
+        regroup_x(5)
 
         ctx.enter_context(tc.manual_schedule(engines={mybir.EngineType.DVE, mybir.EngineType.Pool}))
-        for i in range(TILES + 6):
-            even = i % 2 == 0
-            if i % CHUNK == 0 and i // CHUNK + AHEAD < CHUNKS:
-                load_chunk(i // CHUNK + AHEAD)
-            copy = nc.vector.tensor_copy if i < 2 else nc.scalar.copy
-            diff_on_tensor(i - 4)
-            means(i)
-            square_sums(i)
-            inverse_std(i)
-            times_gamma(i, 0)
-            add_norm0(i - 2)
-            times_gamma(i, 1)
-            add_norm1(i - 2)
-            regroup_x(i + 2, copy)
-            if even:
-                regroup_h(i // 2 + 1, copy=copy)
-            gate(i - 3)
-            if not even:
-                add_h_and_store(i - 6)
-            quantise_x(i + 2)
-            if even:
-                quantise_h(i // 2 + 1)
-            gate_times_diff(i - 4)
-            if even:
-                add_h_and_store(i - 4)
-            diff_on_gpsimd(i + 2)
-            products(i + 1)
-            transpose_x(i + 3)
-            if not even:
-                transpose_h((i + 3) // 2)
+        for q in range(1, PAIRS):
+            e, o = 2 * q, 2 * q + 1
+            if q % 2 == 1 and q // 2 + AHEAD < CHUNKS:
+                load_chunk(q // 2 + AHEAD)
+            diff_on_tensor(e - 4)
+            gate(e - 4)
+            gate(o - 4)
+            times_gamma(e, 0)
+            product(o, 1)
+            square_sum(o, 1)
+            inverse_stds(q)
+            times_gamma(e, 1)
+            add_norm0(e - 2)
+            if q == 1:
+                quantise_x(4)
+                quantise_h(2)
+            gate_times_diff(e - 4)
+            times_gamma(o, 0)
+            add_norm0(o - 2)
+            times_gamma(o, 1)
+            if q == 1:
+                quantise_x(5)
+            transpose_x(e + 4)
+            transpose_h(q + 2)
+            sums_of_blocks(e + 2)
+            regroup_x(e + 4)
+            regroup_h(q + 2)
+            add_norm1(e - 2)
+            odd_diff(o + 2, nc.vector, 256)
+            quantise_x(e + 4)
+            product(e + 2, 0)
+            product(e + 2, 1)
+            means(e + 2)
+            square_sum(e + 2, 0)
+            square_sum(e + 2, 1)
+            add_norm1(o - 2)
+            transpose_x(o + 4)
+            sums_of_blocks(o + 2)
+            product(o + 2, 0)
+            regroup_x(o + 4)
+            means(o + 2)
+            square_sum(o + 2, 0)
+            quantise_h(q + 2)
+            quantise_x(o + 4)
+            gate_times_diff(o - 4)
+            add_h_and_store(nc.gpsimd, e - 4, 2 if q < PAIRS - 1 else 1)
+            odd_diff(o + 2, nc.gpsimd, 0, 256)
+
+        last = TILES - 1
+        gate(last - 3)
+        gate(last - 2)
+        diff_on_tensor(last - 3)
+        add_norm0(last - 1)
+        gate_times_diff(last - 3)
+        add_norm0(last)
+        add_norm1(last - 1)
+        gate(last - 1)
+        gate_times_diff(last - 2)
+        add_norm1(last)
+        gate(last)
+        add_h_and_store(nc.vector, last - 4, 1)
+        diff_on_tensor(last - 1)
+        add_h_and_store(nc.vector, last - 3, 2)
+        gate_times_diff(last - 1)
+        gate_times_diff(last)
+        add_h_and_store(nc.vector, last - 1, 1)
+        add_h_and_store(nc.vector, last, 1)

@@ -263,7 +263,7 @@ def tile_layernormgrucell_pb_t_kernel(tc, x, h, c, W_u, U_u, ln_gamma, ln_beta, 
                 nc.scalar.activation(out=ln1[t][:], in_=ln1[t][:], func=ACT.Sigmoid)
 
         def diff_on_tensor(t):
-            if not 0 <= t < TILES or t % 2 != 0:
+            if not 0 <= t < TILES:
                 return
             diff[t] = psum_one.tile([P, H], F32, name="diff_psum", tag="diff_psum")
             nc.tensor.matmul(out=diff[t][:], lhsT=plus_i[:], rhs=c_of(t), start=True, stop=False)
@@ -284,13 +284,15 @@ def tile_layernormgrucell_pb_t_kernel(tc, x, h, c, W_u, U_u, ln_gamma, ln_beta, 
                 blend[t // 2] = work.tile([P, 2, H], F32, name="blend", tag="blend", bufs=4)
             nc.vector.tensor_tensor(out=blend[t // 2][:, t % 2, :], in0=ln1[t][:], in1=diff[t][:], op=ALU.mult)
 
-        def add_h_and_store(engine, first, n):
+        def add_h_and_store(engine, first, n, parts=1):
             if not 0 <= first < TILES:
                 return
-            y = blend[first // 2][:, first % 2:first % 2 + n, :]
-            h_rows_of = h_chunk[first // CHUNK][:, first % CHUNK:first % CHUNK + n, :]
-            engine.tensor_tensor(out=y, in0=y, in1=h_rows_of, op=ALU.add)
-            nc.sync.dma_start(out=out_rows[:, first:first + n, :], in_=y)
+            for j in range(parts):
+                features = slice(j * H // parts, (j + 1) * H // parts)
+                y = blend[first // 2][:, first % 2:first % 2 + n, features]
+                h_rows_of = h_chunk[first // CHUNK][:, first % CHUNK:first % CHUNK + n, features]
+                engine.tensor_tensor(out=y, in0=y, in1=h_rows_of, op=ALU.add)
+                nc.sync.dma_start(out=out_rows[:, first:first + n, features], in_=y)
 
         ctx.enter_context(tc.manual_schedule(engines={mybir.EngineType.DVE, mybir.EngineType.Pool}))
         transpose_h(0, (0,))
@@ -338,7 +340,7 @@ def tile_layernormgrucell_pb_t_kernel(tc, x, h, c, W_u, U_u, ln_gamma, ln_beta, 
         product(1, 0)
         means(1)
         square_sum(1, 0)
-        odd_diff(1, nc.vector)
+        odd_diff(1, nc.gpsimd)
         times_gamma(0, 0)
         times_gamma(0, 1)
         product(1, 1)
@@ -371,7 +373,6 @@ def tile_layernormgrucell_pb_t_kernel(tc, x, h, c, W_u, U_u, ln_gamma, ln_beta, 
         transpose_x(5)
         regroup_x(5)
 
-        ctx.enter_context(tc.manual_schedule(engines={mybir.EngineType.DVE, mybir.EngineType.Pool}))
         for q in range(1, PAIRS):
             e, o = 2 * q, 2 * q + 1
             if q % 2 == 1 and q // 2 + AHEAD < CHUNKS:
@@ -400,7 +401,8 @@ def tile_layernormgrucell_pb_t_kernel(tc, x, h, c, W_u, U_u, ln_gamma, ln_beta, 
             regroup_x(e + 4)
             regroup_h(q + 2)
             add_norm1(e - 2)
-            odd_diff(o + 2, nc.vector, 256)
+            if q < PAIRS - 2:
+                odd_diff(o + 2, nc.vector, 256)
             quantise_x(e + 4)
             product(e + 2, 0)
             product(e + 2, 1)
@@ -417,8 +419,12 @@ def tile_layernormgrucell_pb_t_kernel(tc, x, h, c, W_u, U_u, ln_gamma, ln_beta, 
             quantise_h(q + 2)
             quantise_x(o + 4)
             gate_times_diff(o - 4)
-            add_h_and_store(nc.gpsimd, e - 4, 2 if q < PAIRS - 1 else 1)
-            odd_diff(o + 2, nc.gpsimd, 0, 256)
+            if q < PAIRS - 1:
+                add_h_and_store(nc.gpsimd, e - 4, 2)
+            else:
+                add_h_and_store(nc.gpsimd, o - 4, 1)
+            if q < PAIRS - 2:
+                odd_diff(o + 2, nc.gpsimd, 0, 256)
 
         last = TILES - 1
         gate(last - 3)
@@ -432,10 +438,11 @@ def tile_layernormgrucell_pb_t_kernel(tc, x, h, c, W_u, U_u, ln_gamma, ln_beta, 
         gate_times_diff(last - 2)
         add_norm1(last)
         gate(last)
-        add_h_and_store(nc.vector, last - 4, 1)
+        add_h_and_store(nc.vector, last - 5, 1)
         diff_on_tensor(last - 1)
-        add_h_and_store(nc.vector, last - 3, 2)
         gate_times_diff(last - 1)
+        diff_on_tensor(last)
+        add_h_and_store(nc.vector, last - 3, 2)
         gate_times_diff(last)
         add_h_and_store(nc.vector, last - 1, 1)
-        add_h_and_store(nc.vector, last, 1)
+        add_h_and_store(nc.vector, last, 1, 2)

@@ -31,7 +31,7 @@ def tile_layernormgrucell_pb_t_kernel(tc, x, h, c, W_u, U_u, ln_gamma, ln_beta, 
         x_pool = ctx.enter_context(tc.tile_pool(name="x_pool", bufs=AHEAD + 1))
         h_pool = ctx.enter_context(tc.tile_pool(name="h_pool", bufs=CHUNKS))
         c_pool = ctx.enter_context(tc.tile_pool(name="c_pool", bufs=AHEAD + 2))
-        front = ctx.enter_context(tc.tile_pool(name="front", bufs=4))
+        front = ctx.enter_context(tc.tile_pool(name="front", bufs=5))
         work = ctx.enter_context(tc.tile_pool(name="work", bufs=4))
         stats = ctx.enter_context(tc.tile_pool(name="stats", bufs=6))
         psum_ring = ctx.enter_context(tc.psum_pool(name="psum_ring", bufs=3))
@@ -269,11 +269,15 @@ def tile_layernormgrucell_pb_t_kernel(tc, x, h, c, W_u, U_u, ln_gamma, ln_beta, 
             nc.tensor.matmul(out=diff[t][:], lhsT=plus_i[:], rhs=c_of(t), start=True, stop=False)
             nc.tensor.matmul(out=diff[t][:], lhsT=minus_i[:], rhs=h_of(t), start=False, stop=True)
 
-        def odd_diff(t, engine, first=0, last=H):
+        def odd_diff(t, engine, first=0, last=H, over=None):
             if not 0 <= t < TILES or t % 2 != 1:
                 return
             if t not in diff:
-                diff[t] = work.tile([P, H], F32, name="diff", tag="diff", bufs=6)
+                if over is None:
+                    odd_c_minus_h = work.tile([P, H], F32, name="diff", tag="diff", bufs=6)
+                    diff[t] = odd_c_minus_h[:]
+                else:
+                    diff[t] = x_grouped[over][:].bitcast(F32)
             engine.tensor_tensor(out=diff[t][:, first:last], in0=c_of(t)[:, first:last], in1=h_of(t)[:, first:last],
                                  op=ALU.subtract)
 
@@ -340,7 +344,6 @@ def tile_layernormgrucell_pb_t_kernel(tc, x, h, c, W_u, U_u, ln_gamma, ln_beta, 
         product(1, 0)
         means(1)
         square_sum(1, 0)
-        odd_diff(1, nc.gpsimd)
         times_gamma(0, 0)
         times_gamma(0, 1)
         product(1, 1)
@@ -360,10 +363,10 @@ def tile_layernormgrucell_pb_t_kernel(tc, x, h, c, W_u, U_u, ln_gamma, ln_beta, 
         square_sum(2, 0)
         square_sum(2, 1)
         regroup_x(3, nc.vector.tensor_copy)
-        odd_diff(3, nc.vector)
         transpose_x(4)
         transpose_h(2)
         quantise_x(3)
+        odd_diff(1, nc.gpsimd, over=3)
         sums_of_blocks(3)
         regroup_x(4, nc.vector.tensor_copy)
         regroup_h(2)
@@ -383,7 +386,6 @@ def tile_layernormgrucell_pb_t_kernel(tc, x, h, c, W_u, U_u, ln_gamma, ln_beta, 
             times_gamma(e, 0)
             product(o, 1)
             square_sum(o, 1)
-            inverse_stds(q)
             times_gamma(e, 1)
             add_norm0(e - 2)
             if q == 1:
@@ -399,9 +401,10 @@ def tile_layernormgrucell_pb_t_kernel(tc, x, h, c, W_u, U_u, ln_gamma, ln_beta, 
             transpose_h(q + 2)
             sums_of_blocks(e + 2)
             regroup_x(e + 4)
+            inverse_stds(q)
             regroup_h(q + 2)
             add_norm1(e - 2)
-            if q < PAIRS - 2:
+            if 1 < q < PAIRS - 3:
                 odd_diff(o + 2, nc.vector, 256)
             quantise_x(e + 4)
             product(e + 2, 0)
@@ -423,8 +426,13 @@ def tile_layernormgrucell_pb_t_kernel(tc, x, h, c, W_u, U_u, ln_gamma, ln_beta, 
                 add_h_and_store(nc.gpsimd, e - 4, 2)
             else:
                 add_h_and_store(nc.gpsimd, o - 4, 1)
-            if q < PAIRS - 2:
+            if q == 1:
+                odd_diff(o, nc.gpsimd, over=o + 4)
+                odd_diff(o + 2, nc.gpsimd)
+            elif q < PAIRS - 2:
                 odd_diff(o + 2, nc.gpsimd, 0, 256)
+            elif q == PAIRS - 2:
+                odd_diff(o, nc.gpsimd, 256)
 
         last = TILES - 1
         gate(last - 3)

@@ -262,10 +262,10 @@ def tile_layernormgrucell_pb_t_kernel(tc, x, h, c, W_u, U_u, ln_gamma, ln_beta, 
             if 0 <= t < TILES:
                 nc.scalar.activation(out=ln1[t][:], in_=ln1[t][:], func=ACT.Sigmoid)
 
-        def diff_on_tensor(t):
+        def diff_on_tensor(t, pool=psum_one, tag="diff_psum"):
             if not 0 <= t < TILES:
                 return
-            diff[t] = psum_one.tile([P, H], F32, name="diff_psum", tag="diff_psum")
+            diff[t] = pool.tile([P, H], F32, name="diff_psum", tag=tag)
             nc.tensor.matmul(out=diff[t][:], lhsT=plus_i[:], rhs=c_of(t), start=True, stop=False)
             nc.tensor.matmul(out=diff[t][:], lhsT=minus_i[:], rhs=h_of(t), start=False, stop=True)
 
@@ -438,6 +438,7 @@ def tile_layernormgrucell_pb_t_kernel(tc, x, h, c, W_u, U_u, ln_gamma, ln_beta, 
         gate(last - 3)
         gate(last - 2)
         diff_on_tensor(last - 3)
+        diff_on_tensor(last, psum_ring, "prod")
         add_norm0(last - 1)
         gate_times_diff(last - 3)
         add_norm0(last)
@@ -449,8 +450,7 @@ def tile_layernormgrucell_pb_t_kernel(tc, x, h, c, W_u, U_u, ln_gamma, ln_beta, 
         add_h_and_store(nc.vector, last - 5, 1)
         diff_on_tensor(last - 1)
         gate_times_diff(last - 1)
-        diff_on_tensor(last)
         add_h_and_store(nc.vector, last - 3, 2)
         gate_times_diff(last)
         add_h_and_store(nc.vector, last - 1, 1)
-        add_h_and_store(nc.vector, last, 1, 2)
+        add_h_and_store(nc.vector, last, 1)

from contextlib import ExitStack

import concourse.mybir as mybir
from concourse.masks import make_identity

F32 = mybir.dt.float32
BF16 = mybir.dt.bfloat16
U32 = mybir.dt.uint32
U8 = mybir.dt.uint8
I32 = mybir.dt.int32
FP8X4 = mybir.dt.float8_e4m3fn_x4
ALU = mybir.AluOpType
ACT = mybir.ActivationFunctionType

P = 128
ROWS, IN, H = 4096, 1024, 512
BANK = 512
TILES = ROWS // P
PAIRS = TILES // 2
CHUNK = 4
CHUNKS = TILES // CHUNK
AHEAD = 3
EPS = 1e-5
FLOPS = 2 * ROWS * H * (H + IN)


def tile_layernormgrucell_pb_t_kernel(tc, x, h, c, W_u, U_u, ln_gamma, ln_beta, out):
    nc = tc.nc
    with ExitStack() as ctx:
        const = ctx.enter_context(tc.tile_pool(name="const", bufs=1))
        x_pool = ctx.enter_context(tc.tile_pool(name="x_pool", bufs=AHEAD + 1))
        h_pool = ctx.enter_context(tc.tile_pool(name="h_pool", bufs=CHUNKS))
        c_pool = ctx.enter_context(tc.tile_pool(name="c_pool", bufs=AHEAD + 2))
        front = ctx.enter_context(tc.tile_pool(name="front", bufs=5))
        work = ctx.enter_context(tc.tile_pool(name="work", bufs=4))
        stats = ctx.enter_context(tc.tile_pool(name="stats", bufs=6))
        psum_ring = ctx.enter_context(tc.psum_pool(name="psum_ring", bufs=3))
        psum_one = ctx.enter_context(tc.psum_pool(name="psum_one", bufs=1))

        x_rows = x.rearrange("(p t) k -> p t k", t=TILES)
        h_rows = h.rearrange("(p t) k -> p t k", t=TILES)
        c_rows = c.rearrange("(p t) k -> p t k", t=TILES)
        out_rows = out.rearrange("(p t) f -> p t f", t=TILES)

        x_chunk, h_chunk, c_chunk = {}, {}, {}

        def load(pool, chunks, rows, width, n, first=0, last=CHUNK):
            if first == 0:
                chunks[n] = pool.tile([P, CHUNK, width], BF16, name="chunk", tag="chunk")
            nc.sync.dma_start(out=chunks[n][:, first:last, :], in_=rows[:, n * CHUNK + first:n * CHUNK + last, :])

        def load_chunk(n):
            load(h_pool, h_chunk, h_rows, H, n)
            if n == 1:
                load(x_pool, x_chunk, x_rows, IN, n)
            load(c_pool, c_chunk, c_rows, H, n)
            if n != 1:
                load(x_pool, x_chunk, x_rows, IN, n)

        def h_of(t):
            return h_chunk[t // CHUNK][:, t % CHUNK, :]

        def c_of(t):
            return c_chunk[t // CHUNK][:, t % CHUNK, :]

        vectors = const.tile([P, 3, H], BF16, name="vectors")
        nc.vector.memset(vectors[:].bitcast(I32), 0)
        load(h_pool, h_chunk, h_rows, H, 0, 0, 1)
        load(x_pool, x_chunk, x_rows, IN, 0, 0, 1)
        u_raw = const.tile([P, 4, IN], BF16, name="u_raw")
        w_raw = const.tile([P, 4, H], BF16, name="w_raw")
        for half in range(2):
            nc.sync.dma_start(out=u_raw[:, 2 * half:2 * half + 2, :],
                              in_=U_u.rearrange("(b p) k -> p b k", p=P)[:, 2 * half:2 * half + 2, :])
        nc.sync.dma_start(out=vectors[0:1, 0:2, :], in_=ln_gamma.rearrange("(o g) f -> o g f", o=1))
        nc.sync.dma_start(out=vectors[0:2, 2, :], in_=ln_beta)
        for half in range(2):
            nc.sync.dma_start(out=w_raw[:, 2 * half:2 * half + 2, :],
                              in_=W_u.rearrange("(b p) k -> p b k", p=P)[:, 2 * half:2 * half + 2, :])
        load(h_pool, h_chunk, h_rows, H, 0, 1, 2)
        load(x_pool, x_chunk, x_rows, IN, 0, 1, 2)
        load(h_pool, h_chunk, h_rows, H, 0, 2, CHUNK)
        load(x_pool, x_chunk, x_rows, IN, 0, 2, CHUNK)
        load(c_pool, c_chunk, c_rows, H, 0)
        for n in range(1, AHEAD):
            load_chunk(n)

        ident = const.tile([P, P], F32, name="ident")
        make_identity(nc, ident[:])
        plus_i = const.tile([P, P], BF16, name="plus_i")
        make_identity(nc, plus_i[:])
        minus_half = const.tile([P, 4], F32, name="minus_half")
        nc.gpsimd.memset(minus_half[:], -0.5)
        eps = const.tile([P, 1], F32, name="eps")
        nc.gpsimd.memset(eps[:], EPS)
        ones = const.tile([P, P], BF16, name="ones")
        nc.vector.memset(ones[:], 1.0)
        minus_i = const.tile([P, P], BF16, name="minus_i")
        nc.vector.tensor_scalar(out=minus_i[:], in0=plus_i[:], scalar1=-1.0, scalar2=None, op0=ALU.mult)

        w_grouped = const.tile([P, 3, 4 * H], BF16, name="w_grouped", align_bytes=64)
        w_words = const.tile([P, 3, H], U32, name="w_words", align_bytes=64)
        w_scales = const.tile([P, 3, H], U8, name="w_scales", align_bytes=64)

        def transpose_weight(n_pass, half, bank, on_scalar):
            raw = (w_raw if n_pass == 0 else u_raw)[:].bitcast(F32)
            first_word = 2 * P * max(n_pass - 1, 0)
            for u in range(2):
                for b in range(2):
                    nc.tensor.transpose(
                        bank[:, (2 * u + b) * P:(2 * u + b + 1) * P],
                        raw[:, 2 * half + b, first_word + u * P:first_word + (u + 1) * P],
                        ident[:],
                    )
            grouped = w_grouped[:].bitcast(F32)[:, n_pass, half * BANK:(half + 1) * BANK]
            copy = nc.scalar.copy if on_scalar else nc.vector.tensor_copy
            copy(out=grouped.rearrange("p (f u) -> p f u", u=2), in_=bank[:].rearrange("p (u f) -> p f u", u=2))

        def quantise_weight(n_pass, half):
            features = slice(half * 2 * P, (half + 1) * 2 * P)
            nc.vector.quantize_mx(out=w_words[:, n_pass, features].bitcast(FP8X4), scales=w_scales[:, n_pass, features],
                                  in_=w_grouped[:, n_pass, half * 2 * H:(half + 1) * 2 * H])

        x_t, h_t, x_grouped, h_grouped, x_words, x_scales, h_words, h_scales = {}, {}, {}, {}, {}, {}, {}, {}
        block_sums, prod0, prod1, neg_mean, sq_sum, rstd, ln0, ln1, diff, blend = {}, {}, {}, {}, {}, {}, {}, {}, {}, {}

        def transpose_x(t):
            if not 0 <= t < TILES:
                return
            words = x_chunk[t // CHUNK][:].bitcast(F32)
            x_t[t] = psum_one.tile([P, BANK], F32, name="x_t", tag="x_t")
            for b in range(4):
                nc.tensor.transpose(x_t[t][:, b * P:(b + 1) * P], words[:, t % CHUNK, b * P:(b + 1) * P], ident[:])

        def transpose_h(pair, parts=(0, 1)):
            if not 0 <= pair < PAIRS:
                return
            h_t[pair] = psum_one.tile([P, BANK], F32, name="h_t", tag="h_t")
            for s in parts:
                t = 2 * pair + s
                words = h_chunk[t // CHUNK][:].bitcast(F32)
                for u in range(2):
                    nc.tensor.transpose(h_t[pair][:, (2 * s + u) * P:(2 * s + u + 1) * P],
                                        words[:, t % CHUNK, u * P:(u + 1) * P], ident[:])

        def regroup_x(t, copy=nc.scalar.copy):
            if not 0 <= t < TILES:
                return
            x_grouped[t] = front.tile([P, IN], BF16, name="x_grouped", tag="x_grouped", align_bytes=64)
            copy(out=x_grouped[t][:].bitcast(F32).rearrange("p (g r u) -> p g r u", g=2, u=2),
                 in_=x_t[t][:].rearrange("p (g u r) -> p g r u", g=2, u=2))

        def regroup_h(pair, parts=(0, 1), copy=nc.scalar.copy):
            if not 0 <= pair < PAIRS:
                return
            if parts[0] == 0:
                h_grouped[pair] = front.tile([P, 2 * H], BF16, name="h_grouped", tag="h_grouped", align_bytes=64)
            words = slice(parts[0] * 2 * P, (parts[-1] + 1) * 2 * P)
            copy(out=h_grouped[pair][:].bitcast(F32)[:, words].rearrange("p (s r u) -> p s r u", u=2, r=P),
                 in_=h_t[pair][:, words].rearrange("p (s u r) -> p s r u", u=2, r=P))

        def quantise_x(t):
            if not 0 <= t < TILES:
                return
            x_words[t] = front.tile([P, 2 * P], U32, name="x_words", tag="x_words", align_bytes=64)
            x_scales[t] = front.tile([P, 2 * P], U8, name="x_scales", tag="x_scales", align_bytes=64)
            nc.vector.quantize_mx(out=x_words[t][:].bitcast(FP8X4), scales=x_scales[t][:], in_=x_grouped[t][:])

        def quantise_h(pair, parts=(0, 1)):
            if not 0 <= pair < PAIRS:
                return
            if parts[0] == 0:
                h_words[pair] = front.tile([P, 2 * P], U32, name="h_words", tag="h_words", align_bytes=64)
                h_scales[pair] = front.tile([P, 2 * P], U8, name="h_scales", tag="h_scales", align_bytes=64)
            rows = slice(parts[0] * P, (parts[-1] + 1) * P)
            nc.vector.quantize_mx(out=h_words[pair][:, rows].bitcast(FP8X4), scales=h_scales[pair][:, rows],
                                  in_=h_grouped[pair][:, parts[0] * H:(parts[-1] + 1) * H])

        def mx_pass(acc, words, scales, n_pass, features, start, stop):
            nc.tensor.matmul_mx(out=acc, lhsT=words.bitcast(FP8X4), lhsT_scale=scales,
                                rhs=w_words[:, n_pass, features].bitcast(FP8X4), rhs_scale=w_scales[:, n_pass, features],
                                start=start, stop=stop)

        def operands_of(t):
            rows_h = slice((t % 2) * P, (t % 2 + 1) * P)
            operands = [(h_words[t // 2][:, rows_h], h_scales[t // 2][:, rows_h], 0)]
            for g in range(2):
                operands.append((x_words[t][:, g * P:(g + 1) * P], x_scales[t][:, g * P:(g + 1) * P], 1 + g))
            return operands

        def sums_of_blocks(t):
            if not 0 <= t < TILES:
                return
            block_sums[t] = psum_one.tile([P, 2 * P], F32, name="block_sums", tag="block_sums")
            for n, (words, scales, n_pass) in list(enumerate(operands_of(t)))[1:] + list(enumerate(operands_of(t)))[:1]:
                for b in range(4):
                    mx_pass(block_sums[t][:, min(n, 1) * P:(min(n, 1) + 1) * P], words, scales, n_pass,
                            slice(b * P, (b + 1) * P), start=(n < 2 and b == 0), stop=(n != 1 and b == 3))

        def product(t, n):
            if not 0 <= t < TILES:
                return
            prod = psum_ring.tile([P, H], F32, name="prod", tag="prod")
            (prod0, prod1)[n][t] = prod
            passes = operands_of(t)[:1] if n == 0 else operands_of(t)[1:]
            for j, (words, scales, n_pass) in enumerate(passes):
                mx_pass(prod[:], words, scales, n_pass, slice(0, H), start=(j == 0), stop=(j == len(passes) - 1))

        def means(t):
            if not 0 <= t < TILES:
                return
            neg_mean[t] = stats.tile([P, 2], F32, name="neg_mean", tag="neg_mean")
            unused = work.tile([P, 2 * P], F32, name="unused", tag="unused", bufs=2)
            for n in range(2):
                nc.scalar.activation(out=unused[:, n * P:(n + 1) * P], in_=block_sums[t][:, n * P:(n + 1) * P],
                                     func=ACT.Identity, scale=-1.0 / H, accum_out=neg_mean[t][:, n:n + 1])

        def square_sum(t, n):
            if not 0 <= t < TILES:
                return
            pair = t // 2
            if t % 2 == 0 and n == 0:
                sq_sum[pair] = stats.tile([P, 4], F32, name="sq_sum", tag="sq_sum")
            if n == 0:
                ln0[t] = work.tile([P, H], F32, name="ln0", tag="ln0", bufs=6)
            else:
                ln1[t] = work.tile([P, H], F32, name="ln1", tag="ln1", bufs=8)
            prod, squares = (prod0[t], ln0[t]) if n == 0 else (prod1[t], ln1[t])
            column = 2 * (t % 2) + n
            nc.scalar.activation(out=squares[:], in_=prod[:], func=ACT.Square, bias=neg_mean[t][:, n:n + 1],
                                 accum_out=sq_sum[pair][:, column:column + 1])

        def inverse_stds(pair):
            if not 0 <= pair < PAIRS:
                return
            var_eps = stats.tile([P, 4], F32, name="var_eps", tag="var_eps")
            rstd[pair] = stats.tile([P, 4], F32, name="rstd", tag="rstd")
            nc.scalar.activation(out=var_eps[:], in_=sq_sum[pair][:], func=ACT.Identity, scale=1.0 / H, bias=eps[:, 0:1])
            nc.gpsimd.tensor_tensor(out=rstd[pair][:], in0=var_eps[:], in1=minus_half[:], op=ALU.pow)

        def rstd_of(t, n):
            return rstd[t // 2][:, 2 * (t % 2) + n:2 * (t % 2) + n + 1]

        def times_gamma(t, n):
            if not 0 <= t < TILES:
                return
            prod, dst = ((prod0[t], ln0[t]), (prod1[t], ln1[t]))[n]
            nc.vector.scalar_tensor_tensor(out=dst[:], in0=prod[:], scalar=neg_mean[t][:, n:n + 1],
                                           in1=gamma[:, n * H:(n + 1) * H], op0=ALU.add, op1=ALU.mult)

        def add_norm0(t):
            if 0 <= t < TILES:
                nc.vector.scalar_tensor_tensor(out=ln0[t][:], in0=ln0[t][:], scalar=rstd_of(t, 0), in1=beta_sum[:],
                                               op0=ALU.mult, op1=ALU.add)

        def add_norm1(t):
            if 0 <= t < TILES:
                nc.vector.scalar_tensor_tensor(out=ln1[t][:], in0=ln1[t][:], scalar=rstd_of(t, 1), in1=ln0[t][:],
                                               op0=ALU.mult, op1=ALU.add)

        def gate(t):
            if 0 <= t < TILES:
                nc.scalar.activation(out=ln1[t][:], in_=ln1[t][:], func=ACT.Sigmoid)

        def diff_on_tensor(t, pool=psum_one, tag="diff_psum"):
            if not 0 <= t < TILES:
                return
            diff[t] = pool.tile([P, H], F32, name="diff_psum", tag=tag)
            nc.tensor.matmul(out=diff[t][:], lhsT=plus_i[:], rhs=c_of(t), start=True, stop=False)
            nc.tensor.matmul(out=diff[t][:], lhsT=minus_i[:], rhs=h_of(t), start=False, stop=True)

        def odd_diff(t, engine, first=0, last=H, over=None):
            if not 0 <= t < TILES or t % 2 != 1:
                return
            if t not in diff:
                if over is None:
                    odd_c_minus_h = work.tile([P, H], F32, name="diff", tag="diff", bufs=6)
                    diff[t] = odd_c_minus_h[:]
                else:
                    diff[t] = x_grouped[over][:].bitcast(F32)
            engine.tensor_tensor(out=diff[t][:, first:last], in0=c_of(t)[:, first:last], in1=h_of(t)[:, first:last],
                                 op=ALU.subtract)

        def gate_times_diff(t):
            if not 0 <= t < TILES:
                return
            if t % 2 == 0:
                blend[t // 2] = work.tile([P, 2, H], F32, name="blend", tag="blend", bufs=4)
            nc.vector.tensor_tensor(out=blend[t // 2][:, t % 2, :], in0=ln1[t][:], in1=diff[t][:], op=ALU.mult)

        def add_h_and_store(engine, first, n, parts=1):
            if not 0 <= first < TILES:
                return
            for j in range(parts):
                features = slice(j * H // parts, (j + 1) * H // parts)
                y = blend[first // 2][:, first % 2:first % 2 + n, features]
                h_rows_of = h_chunk[first // CHUNK][:, first % CHUNK:first % CHUNK + n, features]
                engine.tensor_tensor(out=y, in0=y, in1=h_rows_of, op=ALU.add)
                nc.sync.dma_start(out=out_rows[:, first:first + n, features], in_=y)

        ctx.enter_context(tc.manual_schedule(engines={mybir.EngineType.DVE, mybir.EngineType.Pool}))
        transpose_h(0, (0,))
        transpose_x(0)
        regroup_h(0, (0,))
        regroup_x(0)
        quantise_h(0, (0,))
        quantise_x(0)
        transpose_weight(1, 0, psum_ring.tile([P, BANK], F32, name="w_t0", tag="prod"), True)
        transpose_weight(2, 0, psum_ring.tile([P, BANK], F32, name="w_t1", tag="prod"), False)
        quantise_weight(1, 0)
        transpose_weight(1, 1, psum_ring.tile([P, BANK], F32, name="w_t2", tag="prod"), True)
        quantise_weight(2, 0)
        transpose_weight(2, 1, psum_one.tile([P, BANK], F32, name="w_t3", tag="diff_psum"), False)
        quantise_weight(1, 1)
        transpose_weight(0, 0, psum_one.tile([P, BANK], F32, name="w_t4", tag="beta_sum"), True)
        quantise_weight(2, 1)
        transpose_weight(0, 1, psum_ring.tile([P, BANK], F32, name="w_t5", tag="prod"), True)
        quantise_weight(0, 0)
        gamma = const.tile([P, 2 * H], F32, name="gamma")
        spread = {}
        for n in range(2):
            spread[n] = psum_ring.tile([P, H], F32, name="spread", tag="prod")
            nc.tensor.matmul(out=spread[n][:], lhsT=ones[:], rhs=vectors[:, n, :], start=True, stop=True)
        quantise_weight(0, 1)
        nc.scalar.copy(out=gamma[:, 0:H], in_=spread[0][:])
        beta_sum = psum_one.tile([P, H], F32, name="beta_sum", tag="beta_sum")
        nc.tensor.matmul(out=beta_sum[:], lhsT=ones[:], rhs=vectors[:, 2, :], start=True, stop=True)
        nc.vector.tensor_copy(out=gamma[:, H:2 * H], in_=spread[1][:])
        transpose_x(1)
        transpose_h(0, (1,))
        sums_of_blocks(0)
        product(0, 0)
        product(0, 1)
        regroup_x(1, nc.vector.tensor_copy)
        regroup_h(0, (1,), nc.vector.tensor_copy)
        means(0)
        square_sum(0, 0)
        square_sum(0, 1)
        quantise_x(1)
        quantise_h(0, (1,))
        transpose_x(2)
        transpose_h(1)
        sums_of_blocks(1)
        product(1, 0)
        means(1)
        square_sum(1, 0)
        times_gamma(0, 0)
        times_gamma(0, 1)
        product(1, 1)
        square_sum(1, 1)
        inverse_stds(0)
        regroup_x(2, nc.vector.tensor_copy)
        regroup_h(1, copy=nc.vector.tensor_copy)
        quantise_x(2)
        quantise_h(1)
        transpose_x(3)
        sums_of_blocks(2)
        times_gamma(1, 0)
        times_gamma(1, 1)
        product(2, 0)
        product(2, 1)
        means(2)
        square_sum(2, 0)
        square_sum(2, 1)
        regroup_x(3, nc.vector.tensor_copy)
        transpose_x(4)
        transpose_h(2)
        quantise_x(3)
        odd_diff(1, nc.gpsimd, over=3)
        sums_of_blocks(3)
        regroup_x(4, nc.vector.tensor_copy)
        regroup_h(2)
        product(3, 0)
        means(3)
        square_sum(3, 0)
        transpose_x(5)
        regroup_x(5)

        for q in range(1, PAIRS):
            e, o = 2 * q, 2 * q + 1
            if q % 2 == 1 and q // 2 + AHEAD < CHUNKS:
                load_chunk(q // 2 + AHEAD)
            diff_on_tensor(e - 4)
            gate(e - 4)
            gate(o - 4)
            times_gamma(e, 0)
            product(o, 1)
            square_sum(o, 1)
            times_gamma(e, 1)
            add_norm0(e - 2)
            if q == 1:
                quantise_x(4)
                quantise_h(2)
            gate_times_diff(e - 4)
            times_gamma(o, 0)
            add_norm0(o - 2)
            times_gamma(o, 1)
            if q == 1:
                quantise_x(5)
            transpose_x(e + 4)
            transpose_h(q + 2)
            sums_of_blocks(e + 2)
            regroup_x(e + 4)
            inverse_stds(q)
            regroup_h(q + 2)
            add_norm1(e - 2)
            if 1 < q < PAIRS - 3:
                odd_diff(o + 2, nc.vector, 256)
            quantise_x(e + 4)
            product(e + 2, 0)
            product(e + 2, 1)
            means(e + 2)
            square_sum(e + 2, 0)
            square_sum(e + 2, 1)
            add_norm1(o - 2)
            transpose_x(o + 4)
            sums_of_blocks(o + 2)
            product(o + 2, 0)
            regroup_x(o + 4)
            means(o + 2)
            square_sum(o + 2, 0)
            quantise_h(q + 2)
            quantise_x(o + 4)
            gate_times_diff(o - 4)
            if q < PAIRS - 1:
                add_h_and_store(nc.gpsimd, e - 4, 2)
            else:
                add_h_and_store(nc.gpsimd, o - 4, 1)
            if q == 1:
                odd_diff(o, nc.gpsimd, over=o + 4)
                odd_diff(o + 2, nc.gpsimd)
            elif q < PAIRS - 2:
                odd_diff(o + 2, nc.gpsimd, 0, 256)
            elif q == PAIRS - 2:
                odd_diff(o, nc.gpsimd, 256)

        last = TILES - 1
        gate(last - 3)
        gate(last - 2)
        diff_on_tensor(last - 3)
        diff_on_tensor(last, psum_ring, "prod")
        add_norm0(last - 1)
        gate_times_diff(last - 3)
        add_norm0(last)
        add_norm1(last - 1)
        gate(last - 1)
        gate_times_diff(last - 2)
        add_norm1(last)
        gate(last)
        add_h_and_store(nc.vector, last - 5, 1)
        diff_on_tensor(last - 1)
        gate_times_diff(last - 1)
        add_h_and_store(nc.vector, last - 3, 2)
        gate_times_diff(last)
        add_h_and_store(nc.vector, last - 1, 1)
        add_h_and_store(nc.vector, last, 1)
